import numpy as np
import ml_dtypes


def mxq(x, axis, fmt="e4m3"):
    dtype, down = {"e4m3": (ml_dtypes.float8_e4m3fn, 7), "e5m2": (ml_dtypes.float8_e5m2, 14)}[fmt]
    v = np.moveaxis(np.asarray(x, np.float32).astype(ml_dtypes.bfloat16).astype(np.float64), axis, -1)
    blocks = v.reshape(v.shape[:-1] + (-1, 32))
    amax = np.abs(blocks).max(-1, keepdims=True)
    byte = np.maximum(np.where(amax > 0, np.frexp(amax)[1] - 1 + 127, 0) - down, 1)
    scale = np.exp2(byte - 127.0)
    codes = (blocks / scale).astype(np.float32).astype(dtype).astype(np.float64)
    return np.moveaxis((codes * scale).reshape(v.shape), -1, axis)


WIDE = False


def mx_kscale(k):
    if not WIDE:
        return np.ones(k)
    levels = np.array([10, -10, 5, -5, 0])
    a = np.random.permutation(np.resize(levels, k // 512 * 4)).reshape(k // 512, 4)
    idx = np.arange(k)
    return np.exp2(a[idx // 512, idx % 128 // 32])


BF16 = ml_dtypes.bfloat16


def bf(x):
    return np.asarray(x, np.float32).astype(BF16)


def f64(x):
    return np.asarray(x).astype(np.float64)


E2M1 = np.array([0.0, 0.5, 1.0, 1.5, 2.0, 3.0, 4.0, 6.0, -0.0, -0.5, -1.0, -1.5, -2.0, -3.0, -4.0, -6.0])


def pack_weight(w, fmt):
    k, n = w.shape
    w = f64(bf(w)).reshape(k // 32, 32, n)
    amax = np.abs(w).max(1)
    if fmt == "e4m3":
        byte = np.frexp(amax)[1] - 1 + 127 - 7
    else:
        mant, ex = np.frexp(amax / 6.0)
        byte = np.where(mant > 0.5, ex, ex - 1) + 127
    byte = np.clip(np.where(amax > 0, byte, 1), 1, 254)
    scaled = (w * np.exp2(127.0 - byte)[:, None, :]).reshape(k, n).astype(np.float32)
    by_word = np.ascontiguousarray(scaled.reshape(k // 512, 128, 4, n).transpose(0, 1, 3, 2))
    if fmt == "e4m3":
        words = by_word.astype(ml_dtypes.float8_e4m3fn).view(np.uint8)
    else:
        c = by_word.astype(ml_dtypes.float4_e2m1fn).view(np.uint8) & 0xF
        words = c[..., 0::2] | (c[..., 1::2] << 4)
    return np.ascontiguousarray(words), np.ascontiguousarray(byte.astype(np.uint8).reshape(k // 512, 16, n))


def unpack_weight(words, scales, fmt):
    g, p, n, _ = words.shape
    if fmt == "e4m3":
        vals = np.ascontiguousarray(words).view(ml_dtypes.float8_e4m3fn).astype(np.float64)
    else:
        nib = np.empty((g, p, n, 4), np.uint8)
        nib[..., 0::2] = words & 0xF
        nib[..., 1::2] = words >> 4
        vals = E2M1[nib]
    vals = vals * np.repeat(np.exp2(scales.astype(np.float64) - 127.0), 8, axis=1)[..., None]
    return vals.transpose(0, 1, 3, 2).reshape(g * 512, n)


B, NC, APC, D = 512, 8, 512, 512
H = 2 * D
LN_EPS = 1e-5


def setup_inputs():
    s = mx_kscale(APC)
    t = np.exp2(np.round(np.log2(mx_kscale(H)) / 2))
    tri = bf(np.random.standard_normal((B, APC * NC)) * np.repeat(s, NC))
    W1 = np.random.standard_normal((NC, APC, H)) / np.sqrt(APC) / s[None, :, None] * t
    W1_words, W1_scales = pack_weight(W1.reshape(-1, H), "e4m3")
    b1 = bf(np.random.standard_normal((NC, H)) * 0.1 * t)
    W2 = np.random.standard_normal((NC, H, D)) / np.sqrt(H) / (t * t)[None, :, None]
    W2_words, W2_scales = pack_weight(W2.reshape(-1, D), "e4m3")
    b2 = bf(np.random.standard_normal((NC, D)) * 0.1)
    gamma = bf(1.0 + 0.1 * np.random.standard_normal((NC, D)))
    beta = bf(np.random.standard_normal((NC, D)) * 0.1)
    return {"tri": tri,
            "W1_words": W1_words,
            "W1_scales": W1_scales,
            "b1": b1,
            "W2_words": W2_words,
            "W2_scales": W2_scales,
            "b2": b2,
            "gamma": gamma,
            "beta": beta}


def reference(tri, W1_words, W1_scales, b1, W2_words, W2_scales, b2, gamma, beta):
    tri, b1, b2, gamma, beta = f64(tri), f64(b1), f64(b2), f64(gamma), f64(beta)
    W1 = unpack_weight(W1_words, W1_scales, "e4m3").reshape(NC, APC, H)
    W2 = unpack_weight(W2_words, W2_scales, "e4m3").reshape(NC, H, D)
    b, n_anchors = tri.shape
    n_comp, apc, d = NC, APC, D
    x = np.transpose(tri.reshape(b, apc, n_comp), (2, 0, 1))
    h = (mxq(x, 2, "e4m3") @ W1) + b1[:, None, :]
    h = np.square(np.maximum(h, 0.0))
    y = (mxq(h, 2, "e4m3") @ W2) + b2[:, None, :]
    mu = np.mean(y, axis=-1, keepdims=True)
    var = np.mean(np.square(y - mu), axis=-1, keepdims=True)
    y = (y - mu) * (1.0 / np.sqrt(var + LN_EPS))
    y = y * gamma[:, None, :] + beta[:, None, :]
    return np.transpose(y, (1, 0, 2)).reshape(b, n_comp * d)

@@ -1,0 +1,310 @@
+from contextlib import ExitStack
+
+import concourse.mybir as mybir
+from concourse.masks import make_identity
+
+F32 = mybir.dt.float32
+BF16 = mybir.dt.bfloat16
+I32 = mybir.dt.int32
+U32 = mybir.dt.uint32
+U8 = mybir.dt.uint8
+FP8X4 = mybir.dt.float8_e4m3fn_x4
+ALU = mybir.AluOpType
+ACT = mybir.ActivationFunctionType
+
+P = 128
+PACK = 4
+B = 512
+NC = 8
+APC = 512
+H = 1024
+D = 512
+LN_EPS = 1e-5
+ROW_TILES = B // P
+H_PASSES = H // (P * PACK)
+UNITS = NC * ROW_TILES
+FLOPS = 2 * B * NC * (APC * H + H * D)
+
+
+def tile_patchwork_e_kernel(
+    tc, tri, W1_words, W1_scales, b1, W2_words, W2_scales, b2, gamma, beta, out
+):
+    nc = tc.nc
+    with ExitStack() as ctx:
+        keep = ctx.enter_context(tc.tile_pool(name="keep", bufs=1))
+        work = ctx.enter_context(tc.tile_pool(name="work", bufs=3))
+        psum = ctx.enter_context(tc.psum_pool(name="psum", bufs=1))
+        ctx.enter_context(tc.manual_schedule())
+
+        tri_sb = keep.tile([P, ROW_TILES, NC * APC], BF16)
+        w1_words = keep.tile([P, NC, H], U32, align_bytes=64)
+        w2_words = keep.tile([P, NC * H_PASSES, D], U32, align_bytes=64)
+        w1_scales = keep.tile([P, NC, H], U8, align_bytes=64)
+        w2_scales = keep.tile([P, NC * H_PASSES, D], U8, align_bytes=64)
+        b1_rows = keep.tile([P, NC, H], BF16)
+        b2_rows = keep.tile([P, NC, D], BF16)
+        gamma_rows = keep.tile([P, NC, D], BF16)
+        beta_rows = keep.tile([P, NC, D], BF16)
+        identity = keep.tile([P, P], F32)
+        eps = keep.tile([P, 1], F32)
+        table_warm = keep.tile([P, 1], F32)
+
+        nc.vector.memset(w1_scales[:].bitcast(I32), 0)
+        nc.vector.memset(w2_scales[:].bitcast(I32), 0)
+        nc.vector.memset(eps[:], LN_EPS)
+        make_identity(nc, identity[:])
+        nc.scalar.activation(out=table_warm[:], in_=eps[:], func=ACT.Sqrt)
+
+        def load_rows(r):
+            nc.sync.dma_start(out=tri_sb[:, r, :], in_=tri[r * P : (r + 1) * P, :])
+
+        def load_scales(plane, scales):
+            for quad in range(4):
+                nc.sync.dma_start(
+                    out=plane[32 * quad : 32 * quad + 4, :, :].bitcast(I32),
+                    in_=scales[:, 4 * quad : 4 * quad + 4, :].bitcast(I32).rearrange("g r n -> r g n"),
+                )
+
+        def load_w1(e):
+            nc.sync.dma_start(
+                out=w1_words[:, e, :].bitcast(I32),
+                in_=W1_words[e].rearrange("p n t -> p (n t)").bitcast(I32),
+            )
+            nc.sync.dma_start(out=b1_rows[:, e, :], in_=b1[e].partition_broadcast(P))
+
+        def load_w2(e):
+            passes = slice(e * H_PASSES, (e + 1) * H_PASSES)
+            nc.sync.dma_start(
+                out=w2_words[:, passes, :].bitcast(I32),
+                in_=W2_words[passes].rearrange("g p n t -> p g (n t)").bitcast(I32),
+            )
+            nc.sync.dma_start(out=b2_rows[:, e, :], in_=b2[e].partition_broadcast(P))
+
+        def load_norm(e):
+            nc.sync.dma_start(out=gamma_rows[:, e, :], in_=gamma[e].partition_broadcast(P))
+            nc.sync.dma_start(out=beta_rows[:, e, :], in_=beta[e].partition_broadcast(P))
+
+        load_rows(0)
+        load_scales(w1_scales, W1_scales)
+        load_w1(0)
+        load_rows(1)
+        load_scales(w2_scales, W2_scales)
+        load_w2(0)
+        load_rows(2)
+        load_rows(3)
+        load_norm(0)
+        for e in range(1, NC):
+            load_w1(e)
+            load_w2(e)
+            load_norm(e)
+
+        live = {
+            name: {}
+            for name in (
+                "x_sorted", "x_grouped", "x_codes", "x_scales", "z", "u", "h_grouped",
+                "h_codes", "h_scales", "y", "t", "t_sum", "neg_mean", "sq_sum", "std", "rstd",
+            )
+        }
+
+        def sort_x(unit):
+            e, r = divmod(unit, ROW_TILES)
+            x_sorted = work.tile([P, APC], BF16, bufs=4)
+            nc.gpsimd.tensor_scalar(
+                out=x_sorted[:].rearrange("b (u q c) -> b u q c", u=2, c=2),
+                in0=tri_sb[:, r, :].rearrange("b (q u c e) -> b e u q c", u=2, c=2, e=NC)[:, e],
+                scalar1=1.0,
+                scalar2=0.0,
+                op0=ALU.mult,
+                op1=ALU.add,
+            )
+            live["x_sorted"][unit] = x_sorted
+
+        def transpose_x(unit):
+            words = live["x_sorted"][unit][:].bitcast(F32)
+            x_t = psum.tile([P, 2, P], F32)
+            for u in range(2):
+                nc.tensor.transpose(x_t[:, u, :], words[:, u * P : (u + 1) * P], identity[:])
+            x_grouped = work.tile([P, P * PACK], BF16, align_bytes=64)
+            nc.scalar.copy(
+                out=x_grouped[:].bitcast(F32).rearrange("q (b u) -> q b u", u=2),
+                in_=x_t[:].rearrange("q u b -> q b u"),
+            )
+            live["x_grouped"][unit] = x_grouped
+
+        def quantise_x(unit):
+            x_codes = work.tile([P, P], U32, align_bytes=64)
+            x_scales = work.tile([P, P], U8, align_bytes=64)
+            nc.vector.quantize_mx(
+                out=x_codes[:].bitcast(FP8X4), scales=x_scales[:], in_=live["x_grouped"][unit][:]
+            )
+            live["x_codes"][unit] = x_codes
+            live["x_scales"][unit] = x_scales
+
+        def first_matmul(unit):
+            e = unit // ROW_TILES
+            x_codes = live["x_codes"][unit]
+            x_scales = live["x_scales"][unit]
+            halves = []
+            for g in range(H_PASSES):
+                cols = slice(g * 512, (g + 1) * 512)
+                z = psum.tile([P, 512], F32, bufs=4)
+                nc.tensor.matmul_mx(
+                    out=z[:],
+                    lhsT=x_codes[:].bitcast(FP8X4),
+                    lhsT_scale=x_scales[:],
+                    rhs=w1_words[:, e, cols].bitcast(FP8X4),
+                    rhs_scale=w1_scales[:, e, cols],
+                    start=True,
+                    stop=True,
+                )
+                halves.append(z)
+            live["z"][unit] = halves
+
+        def add_b1(unit):
+            e = unit // ROW_TILES
+            u = work.tile([P, H_PASSES, PACK, P], F32)
+            for g, z in enumerate(live["z"][unit]):
+                nc.vector.tensor_tensor(
+                    out=u[:, g, :, :],
+                    in0=z[:].rearrange("b (q t) -> b t q", t=PACK),
+                    in1=b1_rows[:, e, g * 512 : (g + 1) * 512].rearrange("b (q t) -> b t q", t=PACK),
+                    op=ALU.add,
+                )
+            live["u"][unit] = u
+
+        def relu(unit):
+            flat = live["u"][unit][:].rearrange("b g t q -> b (g t q)")
+            nc.scalar.activation(out=flat, in_=flat, func=ACT.Relu)
+
+        def transpose_h(unit):
+            u = live["u"][unit]
+            h_grouped = work.tile([P, H_PASSES, P, PACK], BF16, align_bytes=64)
+            for g in range(H_PASSES):
+                u_t = psum.tile([P, PACK, P], F32, bufs=2)
+                for t in range(PACK):
+                    nc.tensor.transpose(u_t[:, t, :], u[:, g, t, :], identity[:])
+                nc.scalar.activation(
+                    out=h_grouped[:, g, :, :], in_=u_t[:].rearrange("q t b -> q b t"), func=ACT.Square
+                )
+            live["h_grouped"][unit] = h_grouped
+
+        def quantise_h(unit):
+            h_codes = work.tile([P, H_PASSES * P], U32, align_bytes=64, bufs=2)
+            h_scales = work.tile([P, H_PASSES * P], U8, align_bytes=64, bufs=2)
+            nc.vector.quantize_mx(
+                out=h_codes[:].bitcast(FP8X4),
+                scales=h_scales[:],
+                in_=live["h_grouped"][unit][:].rearrange("q g b t -> q (g b t)"),
+            )
+            live["h_codes"][unit] = h_codes
+            live["h_scales"][unit] = h_scales
+
+        def second_matmul(unit):
+            e = unit // ROW_TILES
+            h_codes = live["h_codes"][unit]
+            h_scales = live["h_scales"][unit]
+            y = psum.tile([P, D], F32)
+            for g in range(H_PASSES):
+                rows = slice(g * P, (g + 1) * P)
+                nc.tensor.matmul_mx(
+                    out=y[:],
+                    lhsT=h_codes[:, rows].bitcast(FP8X4),
+                    lhsT_scale=h_scales[:, rows],
+                    rhs=w2_words[:, e * H_PASSES + g, :].bitcast(FP8X4),
+                    rhs_scale=w2_scales[:, e * H_PASSES + g, :],
+                    start=(g == 0),
+                    stop=(g == H_PASSES - 1),
+                )
+            live["y"][unit] = y
+
+        def add_b2(unit):
+            e = unit // ROW_TILES
+            t = work.tile([P, D], F32, bufs=14)
+            t_sum = work.tile([P, 1], F32)
+            nc.vector.scalar_tensor_tensor(
+                out=t[:],
+                in0=live["y"][unit][:],
+                scalar=1.0,
+                in1=b2_rows[:, e, :],
+                op0=ALU.mult,
+                op1=ALU.add,
+                accum_out=t_sum[:],
+            )
+            live["t"][unit] = t
+            live["t_sum"][unit] = t_sum
+
+        def mean(unit):
+            neg_mean = work.tile([P, 1], F32, bufs=4)
+            nc.vector.tensor_scalar_mul(out=neg_mean[:], in0=live["t_sum"][unit][:], scalar1=-1.0 / D)
+            live["neg_mean"][unit] = neg_mean
+
+        def squares(unit):
+            squared = work.tile([P, D], BF16)
+            sq_sum = work.tile([P, 1], F32)
+            nc.scalar.activation(
+                out=squared[:],
+                in_=live["t"][unit][:],
+                func=ACT.Square,
+                bias=live["neg_mean"][unit][:],
+                accum_out=sq_sum[:],
+            )
+            live["sq_sum"][unit] = sq_sum
+
+        def deviation(unit):
+            std = work.tile([P, 1], F32)
+            nc.scalar.activation(
+                out=std[:], in_=live["sq_sum"][unit][:], func=ACT.Sqrt, scale=1.0 / D, bias=eps[:]
+            )
+            live["std"][unit] = std
+
+        def inverse(unit):
+            rstd = work.tile([P, 1], F32)
+            nc.vector.reciprocal(out=rstd[:], in_=live["std"][unit][:])
+            live["rstd"][unit] = rstd
+
+        def centre_times_gamma(unit):
+            e = unit // ROW_TILES
+            t = live["t"][unit]
+            nc.vector.scalar_tensor_tensor(
+                out=t[:],
+                in0=t[:],
+                scalar=live["neg_mean"][unit][:],
+                in1=gamma_rows[:, e, :],
+                op0=ALU.add,
+                op1=ALU.mult,
+            )
+
+        def scale_plus_beta(unit):
+            e, r = divmod(unit, ROW_TILES)
+            t = live["t"][unit]
+            nc.vector.scalar_tensor_tensor(
+                out=t[:],
+                in0=t[:],
+                scalar=live["rstd"][unit][:],
+                in1=beta_rows[:, e, :],
+                op0=ALU.mult,
+                op1=ALU.add,
+            )
+            nc.sync.dma_start(out=out[r * P : (r + 1) * P, e * D : (e + 1) * D], in_=t[:])
+
+        def run(stage, unit):
+            if 0 <= unit < UNITS:
+                stage(unit)
+
+        for step in range(-4, UNITS + 10):
+            run(sort_x, step + 4)
+            run(add_b1, step - 1)
+            run(squares, step - 6)
+            run(deviation, step - 7)
+            run(transpose_x, step + 2)
+            run(transpose_h, step - 2)
+            run(relu, step - 1)
+            run(first_matmul, step)
+            run(add_b2, step - 4)
+            run(mean, step - 5)
+            run(inverse, step - 8)
+            run(quantise_h, step - 3)
+            run(quantise_x, step + 1)
+            run(second_matmul, step - 3)
+            run(scale_plus_beta, step - 9)
+            run(centre_times_gamma, step - 7)

@@ -53,7 +53,7 @@ def tile_patchwork_e_kernel(
         nc.vector.memset(w2_scales[:].bitcast(I32), 0)
         nc.vector.memset(eps[:], LN_EPS)
         make_identity(nc, identity[:])
-        nc.scalar.activation(out=table_warm[:], in_=eps[:], func=ACT.Sqrt)
+        nc.scalar.activation(out=table_warm[:], in_=eps[:], func=ACT.Abs_reciprocal_sqrt)
 
         def load_rows(r):
             nc.sync.dma_start(out=tri_sb[:, r, :], in_=tri[r * P : (r + 1) * P, :])
@@ -101,8 +101,8 @@ def tile_patchwork_e_kernel(
         live = {
             name: {}
             for name in (
-                "x_sorted", "x_grouped", "x_codes", "x_scales", "z", "u", "h_grouped",
-                "h_codes", "h_scales", "y", "t", "t_sum", "neg_mean", "sq_sum", "std", "rstd",
+                "x_sorted", "x_grouped", "x_codes", "x_scales", "z", "neg_b1", "clamped", "h_grouped",
+                "h_codes", "h_scales", "y", "t", "t_sum", "neg_mean", "sq_sum", "rstd",
             )
         }
 
@@ -160,31 +160,49 @@ def tile_patchwork_e_kernel(
                 halves.append(z)
             live["z"][unit] = halves
 
-        def add_b1(unit):
-            e = unit // ROW_TILES
-            u = work.tile([P, H_PASSES, PACK, P], F32)
-            for g, z in enumerate(live["z"][unit]):
-                nc.vector.tensor_tensor(
-                    out=u[:, g, :, :],
-                    in0=z[:].rearrange("b (q t) -> b t q", t=PACK),
-                    in1=b1_rows[:, e, g * 512 : (g + 1) * 512].rearrange("b (q t) -> b t q", t=PACK),
-                    op=ALU.add,
-                )
-            live["u"][unit] = u
+        def sort_b1(e):
+            neg_b1 = work.tile([P, H_PASSES, PACK, P], F32, bufs=2)
+            nc.gpsimd.tensor_scalar(
+                out=neg_b1[:],
+                in0=b1_rows[:, e, :].rearrange("b (g q t) -> b g t q", g=H_PASSES, t=PACK),
+                scalar1=-1.0,
+                scalar2=0.0,
+                op0=ALU.mult,
+                op1=ALU.add,
+            )
+            live["neg_b1"][e] = neg_b1
 
-        def relu(unit):
-            flat = live["u"][unit][:].rearrange("b g t q -> b (g t q)")
-            nc.scalar.activation(out=flat, in_=flat, func=ACT.Relu)
+        def clamp(unit):
+            e = unit // ROW_TILES
+            clamped = work.tile([P, H_PASSES, PACK, P], F32)
+            for g, z in enumerate(live["z"][unit]):
+                nc.vector.scalar_tensor_tensor(
+                    out=clamped[:, g, :, :],
+                    in0=z[:].rearrange("b (q t) -> b t q", t=PACK),
+                    scalar=-1.0,
+                    in1=b1_rows[:, e, g * 512 : (g + 1) * 512].rearrange("b (q t) -> b t q", t=PACK),
+                    op0=ALU.mult,
+                    op1=ALU.min,
+                )
+            live["clamped"][unit] = clamped
 
         def transpose_h(unit):
-            u = live["u"][unit]
+            clamped = live["clamped"][unit]
+            neg_b1 = live["neg_b1"][unit // ROW_TILES]
             h_grouped = work.tile([P, H_PASSES, P, PACK], BF16, align_bytes=64)
             for g in range(H_PASSES):
-                u_t = psum.tile([P, PACK, P], F32, bufs=2)
+                neg_relu = psum.tile([P, PACK, P], F32, bufs=2)
                 for t in range(PACK):
-                    nc.tensor.transpose(u_t[:, t, :], u[:, g, t, :], identity[:])
+                    nc.tensor.matmul(
+                        out=neg_relu[:, t, :], lhsT=clamped[:, g, t, :], rhs=identity[:],
+                        is_transpose=True, start=True, stop=False,
+                    )
+                    nc.tensor.matmul(
+                        out=neg_relu[:, t, :], lhsT=neg_b1[:, g, t, :], rhs=identity[:],
+                        is_transpose=True, start=False, stop=True,
+                    )
                 nc.scalar.activation(
-                    out=h_grouped[:, g, :, :], in_=u_t[:].rearrange("q t b -> q b t"), func=ACT.Square
+                    out=h_grouped[:, g, :, :], in_=neg_relu[:].rearrange("q t b -> q b t"), func=ACT.Square
                 )
             live["h_grouped"][unit] = h_grouped
 
@@ -219,7 +237,7 @@ def tile_patchwork_e_kernel(
 
         def add_b2(unit):
             e = unit // ROW_TILES
-            t = work.tile([P, D], F32, bufs=14)
+            t = work.tile([P, D], F32, bufs=10)
             t_sum = work.tile([P, 1], F32)
             nc.vector.scalar_tensor_tensor(
                 out=t[:],
@@ -234,8 +252,8 @@ def tile_patchwork_e_kernel(
             live["t_sum"][unit] = t_sum
 
         def mean(unit):
-            neg_mean = work.tile([P, 1], F32, bufs=4)
-            nc.vector.tensor_scalar_mul(out=neg_mean[:], in0=live["t_sum"][unit][:], scalar1=-1.0 / D)
+            neg_mean = work.tile([P, 1], F32)
+            nc.scalar.mul(out=neg_mean[:], in_=live["t_sum"][unit][:], mul=-1.0 / D)
             live["neg_mean"][unit] = neg_mean
 
         def squares(unit):
@@ -250,16 +268,11 @@ def tile_patchwork_e_kernel(
             )
             live["sq_sum"][unit] = sq_sum
 
-        def deviation(unit):
-            std = work.tile([P, 1], F32)
-            nc.scalar.activation(
-                out=std[:], in_=live["sq_sum"][unit][:], func=ACT.Sqrt, scale=1.0 / D, bias=eps[:]
-            )
-            live["std"][unit] = std
-
-        def inverse(unit):
+        def inverse_deviation(unit):
             rstd = work.tile([P, 1], F32)
-            nc.vector.reciprocal(out=rstd[:], in_=live["std"][unit][:])
+            nc.scalar.activation(
+                out=rstd[:], in_=live["sq_sum"][unit][:], func=ACT.Abs_reciprocal_sqrt, scale=1.0 / D, bias=eps[:]
+            )
             live["rstd"][unit] = rstd
 
         def centre_times_gamma(unit):
@@ -291,20 +304,20 @@ def tile_patchwork_e_kernel(
             if 0 <= unit < UNITS:
                 stage(unit)
 
-        for step in range(-4, UNITS + 10):
+        for step in range(-4, UNITS + 7):
+            if (step + 3) % ROW_TILES == 0 and 0 <= (step + 3) // ROW_TILES < NC:
+                sort_b1((step + 3) // ROW_TILES)
             run(sort_x, step + 4)
-            run(add_b1, step - 1)
-            run(squares, step - 6)
-            run(deviation, step - 7)
+            run(clamp, step - 1)
+            run(mean, step - 5)
             run(transpose_x, step + 2)
+            run(squares, step - 5)
             run(transpose_h, step - 2)
-            run(relu, step - 1)
+            run(inverse_deviation, step - 5)
             run(first_matmul, step)
             run(add_b2, step - 4)
-            run(mean, step - 5)
-            run(inverse, step - 8)
             run(quantise_h, step - 3)
             run(quantise_x, step + 1)
             run(second_matmul, step - 3)
-            run(scale_plus_beta, step - 9)
-            run(centre_times_gamma, step - 7)
+            run(scale_plus_beta, step - 6)
+            run(centre_times_gamma, step - 5)

@@ -101,7 +101,7 @@ def tile_patchwork_e_kernel(
         live = {
             name: {}
             for name in (
-                "x_sorted", "x_grouped", "x_codes", "x_scales", "z", "neg_b1", "clamped", "h_grouped",
+                "x_sorted", "x_grouped", "x_codes", "x_scales", "z", "u", "h_grouped",
                 "h_codes", "h_scales", "y", "t", "t_sum", "neg_mean", "sq_sum", "rstd",
             )
         }
@@ -160,55 +160,37 @@ def tile_patchwork_e_kernel(
                 halves.append(z)
             live["z"][unit] = halves
 
-        def sort_b1(e):
-            neg_b1 = work.tile([P, H_PASSES, PACK, P], F32, bufs=2)
-            nc.gpsimd.tensor_scalar(
-                out=neg_b1[:],
-                in0=b1_rows[:, e, :].rearrange("b (g q t) -> b g t q", g=H_PASSES, t=PACK),
-                scalar1=-1.0,
-                scalar2=0.0,
-                op0=ALU.mult,
-                op1=ALU.add,
-            )
-            live["neg_b1"][e] = neg_b1
-
-        def clamp(unit):
+        def add_b1(unit):
             e = unit // ROW_TILES
-            clamped = work.tile([P, H_PASSES, PACK, P], F32)
+            u = work.tile([P, H_PASSES, PACK, P], F32, bufs=4)
             for g, z in enumerate(live["z"][unit]):
-                nc.vector.scalar_tensor_tensor(
-                    out=clamped[:, g, :, :],
+                nc.vector.tensor_tensor(
+                    out=u[:, g, :, :],
                     in0=z[:].rearrange("b (q t) -> b t q", t=PACK),
-                    scalar=-1.0,
                     in1=b1_rows[:, e, g * 512 : (g + 1) * 512].rearrange("b (q t) -> b t q", t=PACK),
-                    op0=ALU.mult,
-                    op1=ALU.min,
+                    op=ALU.add,
                 )
-            live["clamped"][unit] = clamped
+            live["u"][unit] = u
 
-        def transpose_h(unit):
-            clamped = live["clamped"][unit]
-            neg_b1 = live["neg_b1"][unit // ROW_TILES]
-            h_grouped = work.tile([P, H_PASSES, P, PACK], BF16, align_bytes=64)
-            for g in range(H_PASSES):
-                neg_relu = psum.tile([P, PACK, P], F32, bufs=2)
-                for t in range(PACK):
-                    nc.tensor.matmul(
-                        out=neg_relu[:, t, :], lhsT=clamped[:, g, t, :], rhs=identity[:],
-                        is_transpose=True, start=True, stop=False,
-                    )
-                    nc.tensor.matmul(
-                        out=neg_relu[:, t, :], lhsT=neg_b1[:, g, t, :], rhs=identity[:],
-                        is_transpose=True, start=False, stop=True,
-                    )
-                nc.scalar.activation(
-                    out=h_grouped[:, g, :, :], in_=neg_relu[:].rearrange("q t b -> q b t"), func=ACT.Square
-                )
-            live["h_grouped"][unit] = h_grouped
+        def relu(unit):
+            flat = live["u"][unit][:].rearrange("b g t q -> b (g t q)")
+            nc.scalar.activation(out=flat, in_=flat, func=ACT.Relu)
+
+        def transpose_h(unit, g):
+            u = live["u"][unit]
+            if g == 0:
+                h_grouped = work.tile([P, H_PASSES, P, PACK], BF16, align_bytes=64)
+                live["h_grouped"][unit] = h_grouped
+            u_t = psum.tile([P, PACK, P], F32, bufs=2)
+            for t in range(PACK):
+                nc.tensor.transpose(u_t[:, t, :], u[:, g, t, :], identity[:])
+            nc.scalar.activation(
+                out=live["h_grouped"][unit][:, g, :, :], in_=u_t[:].rearrange("q t b -> q b t"), func=ACT.Square
+            )
 
         def quantise_h(unit):
-            h_codes = work.tile([P, H_PASSES * P], U32, align_bytes=64, bufs=2)
-            h_scales = work.tile([P, H_PASSES * P], U8, align_bytes=64, bufs=2)
+            h_codes = work.tile([P, H_PASSES * P], U32, align_bytes=64)
+            h_scales = work.tile([P, H_PASSES * P], U8, align_bytes=64)
             nc.vector.quantize_mx(
                 out=h_codes[:].bitcast(FP8X4),
                 scales=h_scales[:],
@@ -253,7 +235,7 @@ def tile_patchwork_e_kernel(
 
         def mean(unit):
             neg_mean = work.tile([P, 1], F32)
-            nc.scalar.mul(out=neg_mean[:], in_=live["t_sum"][unit][:], mul=-1.0 / D)
+            nc.vector.tensor_scalar_mul(out=neg_mean[:], in0=live["t_sum"][unit][:], scalar1=-1.0 / D)
             live["neg_mean"][unit] = neg_mean
 
         def squares(unit):
@@ -300,24 +282,24 @@ def tile_patchwork_e_kernel(
             )
             nc.sync.dma_start(out=out[r * P : (r + 1) * P, e * D : (e + 1) * D], in_=t[:])
 
-        def run(stage, unit):
+        def run(stage, unit, *more):
             if 0 <= unit < UNITS:
-                stage(unit)
+                stage(unit, *more)
 
-        for step in range(-4, UNITS + 7):
-            if (step + 3) % ROW_TILES == 0 and 0 <= (step + 3) // ROW_TILES < NC:
-                sort_b1((step + 3) // ROW_TILES)
+        for step in range(-4, UNITS + 9):
             run(sort_x, step + 4)
-            run(clamp, step - 1)
-            run(mean, step - 5)
+            run(add_b1, step - 1)
+            run(relu, step - 2)
+            run(squares, step - 7)
             run(transpose_x, step + 2)
-            run(squares, step - 5)
-            run(transpose_h, step - 2)
-            run(inverse_deviation, step - 5)
+            run(transpose_h, step - 3, 0)
             run(first_matmul, step)
-            run(add_b2, step - 4)
-            run(quantise_h, step - 3)
+            run(transpose_h, step - 3, 1)
+            run(inverse_deviation, step - 7)
+            run(add_b2, step - 6)
+            run(quantise_h, step - 4)
             run(quantise_x, step + 1)
-            run(second_matmul, step - 3)
-            run(scale_plus_beta, step - 6)
-            run(centre_times_gamma, step - 5)
+            run(mean, step - 6)
+            run(second_matmul, step - 5)
+            run(scale_plus_beta, step - 8)
+            run(centre_times_gamma, step - 7)

@@ -22,7 +22,8 @@ D = 512
 LN_EPS = 1e-5
 ROW_TILES = B // P
 H_PASSES = H // (P * PACK)
-UNITS = NC * ROW_TILES
+PLANES = 4
+ITEMS = NC * ROW_TILES
 FLOPS = 2 * B * NC * (APC * H + H * D)
 
 
@@ -39,9 +40,11 @@ def tile_patchwork_e_kernel(
         tri_sb = keep.tile([P, ROW_TILES, NC * APC], BF16)
         w1_words = keep.tile([P, NC, H], U32, align_bytes=64)
         w2_words = keep.tile([P, NC * H_PASSES, D], U32, align_bytes=64)
-        w1_scales = keep.tile([P, NC, H], U8, align_bytes=64)
-        w2_scales = keep.tile([P, NC * H_PASSES, D], U8, align_bytes=64)
-        b1_rows = keep.tile([P, NC, H], BF16)
+        w1_scales = keep.tile([P, NC // PLANES, H], U8, align_bytes=64)
+        w1_scales_sorted = keep.tile([P, NC // PLANES, H], U8, align_bytes=64)
+        w2_scales = keep.tile([P, NC * H_PASSES // PLANES, D], U8, align_bytes=64)
+        b1_rows = keep.tile([P, H // H_PASSES], BF16)
+        b1_cols = keep.tile([P, NC * H_PASSES, PACK], F32)
         b2_rows = keep.tile([P, NC, D], BF16)
         gamma_rows = keep.tile([P, NC, D], BF16)
         beta_rows = keep.tile([P, NC, D], BF16)
@@ -49,6 +52,7 @@ def tile_patchwork_e_kernel(
         eps = keep.tile([P, 1], F32)
         table_warm = keep.tile([P, 1], F32)
 
+        nc.vector.memset(b1_rows[:], 0.0)
         nc.vector.memset(w1_scales[:].bitcast(I32), 0)
         nc.vector.memset(w2_scales[:].bitcast(I32), 0)
         nc.vector.memset(eps[:], LN_EPS)
@@ -58,11 +62,11 @@ def tile_patchwork_e_kernel(
         def load_rows(r):
             nc.sync.dma_start(out=tri_sb[:, r, :], in_=tri[r * P : (r + 1) * P, :])
 
-        def load_scales(plane, scales):
+        def load_scales(tile, scales, group):
             for quad in range(4):
                 nc.sync.dma_start(
-                    out=plane[32 * quad : 32 * quad + 4, :, :].bitcast(I32),
-                    in_=scales[:, 4 * quad : 4 * quad + 4, :].bitcast(I32).rearrange("g r n -> r g n"),
+                    out=tile[32 * quad : 32 * quad + 4 * PLANES, group, :].bitcast(I32),
+                    in_=scales[PLANES * group : PLANES * (group + 1), 4 * quad : 4 * quad + 4, :].bitcast(I32),
                 )
 
         def load_w1(e):
@@ -70,7 +74,6 @@ def tile_patchwork_e_kernel(
                 out=w1_words[:, e, :].bitcast(I32),
                 in_=W1_words[e].rearrange("p n t -> p (n t)").bitcast(I32),
             )
-            nc.sync.dma_start(out=b1_rows[:, e, :], in_=b1[e].partition_broadcast(P))
 
         def load_w2(e):
             passes = slice(e * H_PASSES, (e + 1) * H_PASSES)
@@ -78,36 +81,70 @@ def tile_patchwork_e_kernel(
                 out=w2_words[:, passes, :].bitcast(I32),
                 in_=W2_words[passes].rearrange("g p n t -> p g (n t)").bitcast(I32),
             )
-            nc.sync.dma_start(out=b2_rows[:, e, :], in_=b2[e].partition_broadcast(P))
 
         def load_norm(e):
+            nc.sync.dma_start(out=b2_rows[:, e, :], in_=b2[e].partition_broadcast(P))
             nc.sync.dma_start(out=gamma_rows[:, e, :], in_=gamma[e].partition_broadcast(P))
             nc.sync.dma_start(out=beta_rows[:, e, :], in_=beta[e].partition_broadcast(P))
 
         load_rows(0)
-        load_scales(w1_scales, W1_scales)
+        nc.sync.dma_start(
+            out=b1_rows[: NC * H_PASSES, :], in_=b1.rearrange("e (g c) -> (e g) c", g=H_PASSES)
+        )
+        load_scales(w1_scales, W1_scales, 0)
         load_w1(0)
-        load_rows(1)
-        load_scales(w2_scales, W2_scales)
+        for r in range(1, ROW_TILES):
+            load_rows(r)
+        load_scales(w1_scales, W1_scales, 1)
+        for group in range(NC * H_PASSES // PLANES):
+            load_scales(w2_scales, W2_scales, group)
         load_w2(0)
-        load_rows(2)
-        load_rows(3)
         load_norm(0)
-        for e in range(1, NC):
-            load_w1(e)
-            load_w2(e)
-            load_norm(e)
+        load_w1(1)
 
         live = {
             name: {}
             for name in (
-                "x_sorted", "x_grouped", "x_codes", "x_scales", "z", "u", "h_grouped",
+                "w1", "x_sorted", "x_t", "x_grouped", "x_codes", "x_scales", "z", "r", "h_grouped",
                 "h_codes", "h_scales", "y", "t", "t_sum", "neg_mean", "sq_sum", "rstd",
             )
         }
 
-        def sort_x(unit):
-            e, r = divmod(unit, ROW_TILES)
+        def stream_weights(e):
+            if 0 < e < NC:
+                load_w2(e)
+                load_norm(e)
+            if e + 1 < NC:
+                load_w1(e + 1)
+
+        def turn_b1():
+            words = b1_rows[:].bitcast(F32)
+            b1_t = psum.tile([P, 2, P], F32, name="x_t")
+            for u in range(2):
+                nc.tensor.transpose(b1_t[:, u, :], words[:, u::2], identity[:])
+            nc.vector.tensor_copy(
+                out=b1_cols[:].rearrange("q r (u c) -> q r u c", c=2),
+                in_=b1_t[:].rearrange("q u r -> q (u r)").bitcast(BF16).rearrange(
+                    "q (u r c) -> q r u c", u=2, c=2
+                )[:, : NC * H_PASSES],
+            )
+
+        def sort_w1_scales(group):
+            nc.vector.tensor_copy(
+                out=w1_scales_sorted[:, group, :].rearrange("p (g t q) -> p g t q", t=PACK, q=P),
+                in_=w1_scales[:, group, :].rearrange("p (g q t) -> p g t q", t=PACK, q=P),
+            )
+
+        def sort_w1(e):
+            w1 = work.tile([P, H], U32, align_bytes=64, bufs=2)
+            nc.gpsimd.tensor_copy(
+                out=w1[:].bitcast(I32).rearrange("p (g t q) -> p g t q", t=PACK, q=P),
+                in_=w1_words[:, e, :].bitcast(I32).rearrange("p (g q t) -> p g t q", t=PACK, q=P),
+            )
+            live["w1"][e] = w1
+
+        def sort_x(n):
+            e, r = divmod(n, ROW_TILES)
             x_sorted = work.tile([P, APC], BF16, bufs=4)
             nc.gpsimd.tensor_scalar(
                 out=x_sorted[:].rearrange("b (u q c) -> b u q c", u=2, c=2),
@@ -117,189 +154,227 @@ def tile_patchwork_e_kernel(
                 op0=ALU.mult,
                 op1=ALU.add,
             )
-            live["x_sorted"][unit] = x_sorted
+            live["x_sorted"][n] = x_sorted
 
-        def transpose_x(unit):
-            words = live["x_sorted"][unit][:].bitcast(F32)
+        def transpose_x(n):
+            words = live["x_sorted"][n][:].bitcast(F32)
             x_t = psum.tile([P, 2, P], F32)
             for u in range(2):
                 nc.tensor.transpose(x_t[:, u, :], words[:, u * P : (u + 1) * P], identity[:])
+            live["x_t"][n] = x_t
+
+        def group_x(n):
             x_grouped = work.tile([P, P * PACK], BF16, align_bytes=64)
             nc.scalar.copy(
                 out=x_grouped[:].bitcast(F32).rearrange("q (b u) -> q b u", u=2),
-                in_=x_t[:].rearrange("q u b -> q b u"),
+                in_=live["x_t"][n][:].rearrange("q u b -> q b u"),
             )
-            live["x_grouped"][unit] = x_grouped
+            live["x_grouped"][n] = x_grouped
 
-        def quantise_x(unit):
-            x_codes = work.tile([P, P], U32, align_bytes=64)
-            x_scales = work.tile([P, P], U8, align_bytes=64)
+        def quantise_x(n):
+            e, r = divmod(n, ROW_TILES)
+            if r == 0:
+                x_codes = work.tile([P, B], U32, align_bytes=64)
+                x_scales = work.tile([P, B], U8, align_bytes=64)
+                live["x_codes"][e] = x_codes
+                live["x_scales"][e] = x_scales
+            rows = slice(r * P, (r + 1) * P)
             nc.vector.quantize_mx(
-                out=x_codes[:].bitcast(FP8X4), scales=x_scales[:], in_=live["x_grouped"][unit][:]
+                out=live["x_codes"][e][:, rows].bitcast(FP8X4),
+                scales=live["x_scales"][e][:, rows],
+                in_=live["x_grouped"][n][:],
             )
-            live["x_codes"][unit] = x_codes
-            live["x_scales"][unit] = x_scales
 
-        def first_matmul(unit):
-            e = unit // ROW_TILES
-            x_codes = live["x_codes"][unit]
-            x_scales = live["x_scales"][unit]
-            halves = []
-            for g in range(H_PASSES):
-                cols = slice(g * 512, (g + 1) * 512)
-                z = psum.tile([P, 512], F32, bufs=4)
+        def first_matmul(n):
+            e, i = divmod(n, ROW_TILES)
+            group, plane = divmod(e, PLANES)
+            x_codes = live["x_codes"][e]
+            x_scales = live["x_scales"][e]
+            pair = []
+            for j in (2 * i, 2 * i + 1):
+                cols = slice(j * P, (j + 1) * P)
+                z = psum.tile([P, B], F32, bufs=4)
                 nc.tensor.matmul_mx(
                     out=z[:],
-                    lhsT=x_codes[:].bitcast(FP8X4),
-                    lhsT_scale=x_scales[:],
-                    rhs=w1_words[:, e, cols].bitcast(FP8X4),
-                    rhs_scale=w1_scales[:, e, cols],
+                    lhsT=live["w1"][e][:, cols].bitcast(FP8X4),
+                    lhsT_scale=w1_scales_sorted[4 * plane : P, group, cols],
+                    rhs=x_codes[:].bitcast(FP8X4),
+                    rhs_scale=x_scales[:],
                     start=True,
                     stop=True,
                 )
-                halves.append(z)
-            live["z"][unit] = halves
+                pair.append(z)
+            live["z"][n] = pair
 
-        def add_b1(unit):
-            e = unit // ROW_TILES
-            u = work.tile([P, H_PASSES, PACK, P], F32, bufs=4)
-            for g, z in enumerate(live["z"][unit]):
-                nc.vector.tensor_tensor(
-                    out=u[:, g, :, :],
-                    in0=z[:].rearrange("b (q t) -> b t q", t=PACK),
-                    in1=b1_rows[:, e, g * 512 : (g + 1) * 512].rearrange("b (q t) -> b t q", t=PACK),
-                    op=ALU.add,
-                )
-            live["u"][unit] = u
+        def relu_on_vector(n):
+            e, i = divmod(n, ROW_TILES)
+            g, half = divmod(i, 2)
+            if half == 0:
+                r = work.tile([P, PACK, B], F32)
+                live["r"][n // 2] = r
+            t = 2 * half
+            nc.vector.tensor_scalar(
+                out=live["r"][n // 2][:, t, :],
+                in0=live["z"][n][0][:],
+                scalar1=b1_cols[:, e * H_PASSES + g, t : t + 1],
+                scalar2=0.0,
+                op0=ALU.add,
+                op1=ALU.max,
+            )
 
-        def relu(unit):
-            flat = live["u"][unit][:].rearrange("b g t q -> b (g t q)")
-            nc.scalar.activation(out=flat, in_=flat, func=ACT.Relu)
-
-        def transpose_h(unit, g):
-            u = live["u"][unit]
-            if g == 0:
-                h_grouped = work.tile([P, H_PASSES, P, PACK], BF16, align_bytes=64)
-                live["h_grouped"][unit] = h_grouped
-            u_t = psum.tile([P, PACK, P], F32, bufs=2)
-            for t in range(PACK):
-                nc.tensor.transpose(u_t[:, t, :], u[:, g, t, :], identity[:])
+        def relu_on_scalar(n):
+            e, i = divmod(n, ROW_TILES)
+            g, half = divmod(i, 2)
+            t = 2 * half + 1
             nc.scalar.activation(
-                out=live["h_grouped"][unit][:, g, :, :], in_=u_t[:].rearrange("q t b -> q b t"), func=ACT.Square
+                out=live["r"][n // 2][:, t, :],
+                in_=live["z"][n][1][:],
+                func=ACT.Relu,
+                bias=b1_cols[:, e * H_PASSES + g, t : t + 1],
             )
 
-        def quantise_h(unit):
-            h_codes = work.tile([P, H_PASSES * P], U32, align_bytes=64)
-            h_scales = work.tile([P, H_PASSES * P], U8, align_bytes=64)
+        def square(n):
+            half = n % 2
+            rows = slice(half * 2 * P, (half + 1) * 2 * P)
+            h_grouped = work.tile([P, 2 * P, PACK], BF16, align_bytes=64)
+            nc.scalar.activation(
+                out=h_grouped[:],
+                in_=live["r"][n // 2][:, :, rows].rearrange("q t b -> q b t"),
+                func=ACT.Square,
+            )
+            live["h_grouped"][n] = h_grouped
+
+        def quantise_h(n):
+            e, i = divmod(n, ROW_TILES)
+            g, half = divmod(i, 2)
+            if i == 0:
+                h_codes = work.tile([P, H_PASSES, B], U32, align_bytes=64)
+                h_scales = work.tile([P, H_PASSES, B], U8, align_bytes=64)
+                live["h_codes"][e] = h_codes
+                live["h_scales"][e] = h_scales
+            rows = slice(half * 2 * P, (half + 1) * 2 * P)
             nc.vector.quantize_mx(
-                out=h_codes[:].bitcast(FP8X4),
-                scales=h_scales[:],
-                in_=live["h_grouped"][unit][:].rearrange("q g b t -> q (g b t)"),
+                out=live["h_codes"][e][:, g, rows].bitcast(FP8X4),
+                scales=live["h_scales"][e][:, g, rows],
+                in_=live["h_grouped"][n][:].rearrange("q b t -> q (b t)"),
             )
-            live["h_codes"][unit] = h_codes
-            live["h_scales"][unit] = h_scales
 
-        def second_matmul(unit):
-            e = unit // ROW_TILES
-            h_codes = live["h_codes"][unit]
-            h_scales = live["h_scales"][unit]
-            y = psum.tile([P, D], F32)
+        def second_matmul(n):
+            e, r = divmod(n, ROW_TILES)
+            rows = slice(r * P, (r + 1) * P)
+            y = psum.tile([P, D], F32, bufs=3)
             for g in range(H_PASSES):
-                rows = slice(g * P, (g + 1) * P)
+                group, plane = divmod(e * H_PASSES + g, PLANES)
                 nc.tensor.matmul_mx(
                     out=y[:],
-                    lhsT=h_codes[:, rows].bitcast(FP8X4),
-                    lhsT_scale=h_scales[:, rows],
+                    lhsT=live["h_codes"][e][:, g, rows].bitcast(FP8X4),
+                    lhsT_scale=live["h_scales"][e][:, g, rows],
                     rhs=w2_words[:, e * H_PASSES + g, :].bitcast(FP8X4),
-                    rhs_scale=w2_scales[:, e * H_PASSES + g, :],
+                    rhs_scale=w2_scales[4 * plane : P, group, :],
                     start=(g == 0),
                     stop=(g == H_PASSES - 1),
                 )
-            live["y"][unit] = y
+            live["y"][n] = y
 
-        def add_b2(unit):
-            e = unit // ROW_TILES
-            t = work.tile([P, D], F32, bufs=10)
+        def add_b2(n):
+            e = n // ROW_TILES
+            t = work.tile([P, D], F32, bufs=8)
             t_sum = work.tile([P, 1], F32)
             nc.vector.scalar_tensor_tensor(
                 out=t[:],
-                in0=live["y"][unit][:],
+                in0=live["y"][n][:],
                 scalar=1.0,
                 in1=b2_rows[:, e, :],
                 op0=ALU.mult,
                 op1=ALU.add,
                 accum_out=t_sum[:],
             )
-            live["t"][unit] = t
-            live["t_sum"][unit] = t_sum
+            live["t"][n] = t
+            live["t_sum"][n] = t_sum
 
-        def mean(unit):
+        def mean(n):
             neg_mean = work.tile([P, 1], F32)
-            nc.vector.tensor_scalar_mul(out=neg_mean[:], in0=live["t_sum"][unit][:], scalar1=-1.0 / D)
-            live["neg_mean"][unit] = neg_mean
+            nc.gpsimd.tensor_scalar(
+                out=neg_mean[:],
+                in0=live["t_sum"][n][:],
+                scalar1=-1.0 / D,
+                scalar2=0.0,
+                op0=ALU.mult,
+                op1=ALU.add,
+            )
+            live["neg_mean"][n] = neg_mean
 
-        def squares(unit):
+        def squares(n):
             squared = work.tile([P, D], BF16)
             sq_sum = work.tile([P, 1], F32)
             nc.scalar.activation(
                 out=squared[:],
-                in_=live["t"][unit][:],
+                in_=live["t"][n][:],
                 func=ACT.Square,
-                bias=live["neg_mean"][unit][:],
+                bias=live["neg_mean"][n][:],
                 accum_out=sq_sum[:],
             )
-            live["sq_sum"][unit] = sq_sum
+            live["sq_sum"][n] = sq_sum
 
-        def inverse_deviation(unit):
+        def inverse_deviation(n):
             rstd = work.tile([P, 1], F32)
             nc.scalar.activation(
-                out=rstd[:], in_=live["sq_sum"][unit][:], func=ACT.Abs_reciprocal_sqrt, scale=1.0 / D, bias=eps[:]
+                out=rstd[:], in_=live["sq_sum"][n][:], func=ACT.Abs_reciprocal_sqrt, scale=1.0 / D, bias=eps[:]
             )
-            live["rstd"][unit] = rstd
+            live["rstd"][n] = rstd
 
-        def centre_times_gamma(unit):
-            e = unit // ROW_TILES
-            t = live["t"][unit]
+        def centre_times_gamma(n):
+            e = n // ROW_TILES
+            t = live["t"][n]
             nc.vector.scalar_tensor_tensor(
                 out=t[:],
                 in0=t[:],
-                scalar=live["neg_mean"][unit][:],
+                scalar=live["neg_mean"][n][:],
                 in1=gamma_rows[:, e, :],
                 op0=ALU.add,
                 op1=ALU.mult,
             )
 
-        def scale_plus_beta(unit):
-            e, r = divmod(unit, ROW_TILES)
-            t = live["t"][unit]
+        def scale_plus_beta(n):
+            e, r = divmod(n, ROW_TILES)
+            t = live["t"][n]
             nc.vector.scalar_tensor_tensor(
                 out=t[:],
                 in0=t[:],
-                scalar=live["rstd"][unit][:],
+                scalar=live["rstd"][n][:],
                 in1=beta_rows[:, e, :],
                 op0=ALU.mult,
                 op1=ALU.add,
             )
             nc.sync.dma_start(out=out[r * P : (r + 1) * P, e * D : (e + 1) * D], in_=t[:])
 
-        def run(stage, unit, *more):
-            if 0 <= unit < UNITS:
-                stage(unit, *more)
+        def run(stage, n):
+            if 0 <= n < ITEMS:
+                stage(n)
 
-        for step in range(-4, UNITS + 9):
-            run(sort_x, step + 4)
-            run(add_b1, step - 1)
-            run(relu, step - 2)
-            run(squares, step - 7)
-            run(transpose_x, step + 2)
-            run(transpose_h, step - 3, 0)
+        turn_b1()
+        sort_w1_scales(0)
+        for step in range(-8, ITEMS + 11):
+            if step >= 0 and step % ROW_TILES == 0:
+                stream_weights(step // ROW_TILES + 1)
+            run(sort_x, step + 8)
+            run(relu_on_vector, step - 1)
+            run(relu_on_scalar, step - 1)
+            run(squares, step - 9)
+            run(transpose_x, step + 6)
+            run(second_matmul, step - 7)
             run(first_matmul, step)
-            run(transpose_h, step - 3, 1)
-            run(inverse_deviation, step - 7)
-            run(add_b2, step - 6)
+            run(square, step - 3)
+            run(inverse_deviation, step - 9)
+            run(group_x, step + 6)
+            run(add_b2, step - 8)
             run(quantise_h, step - 4)
-            run(quantise_x, step + 1)
-            run(mean, step - 6)
-            run(second_matmul, step - 5)
-            run(scale_plus_beta, step - 8)
-            run(centre_times_gamma, step - 7)
+            run(quantise_x, step + 5)
+            run(mean, step - 8)
+            run(scale_plus_beta, step - 10)
+            run(centre_times_gamma, step - 9)
+            ahead, i = divmod(step + 2, ROW_TILES)
+            if i == 0 and 0 <= ahead < NC:
+                sort_w1(ahead)
+            if step == 2:
+                sort_w1_scales(1)

@@ -82,25 +82,35 @@ def tile_patchwork_e_kernel(
                 in_=W2_words[passes].rearrange("g p n t -> p g (n t)").bitcast(I32),
             )
 
-        def load_norm(e):
-            nc.sync.dma_start(out=b2_rows[:, e, :], in_=b2[e].partition_broadcast(P))
-            nc.sync.dma_start(out=gamma_rows[:, e, :], in_=gamma[e].partition_broadcast(P))
-            nc.sync.dma_start(out=beta_rows[:, e, :], in_=beta[e].partition_broadcast(P))
+        def load_norm(rows, param):
+            nc.sync.dma_start(
+                out=rows[:].rearrange("p e n -> p (e n)"), in_=param.rearrange("e n -> (e n)").partition_broadcast(P)
+            )
 
         load_rows(0)
+        load_rows(1)
         nc.sync.dma_start(
             out=b1_rows[: NC * H_PASSES, :], in_=b1.rearrange("e (g c) -> (e g) c", g=H_PASSES)
         )
         load_scales(w1_scales, W1_scales, 0)
         load_w1(0)
-        for r in range(1, ROW_TILES):
-            load_rows(r)
-        load_scales(w1_scales, W1_scales, 1)
-        for group in range(NC * H_PASSES // PLANES):
-            load_scales(w2_scales, W2_scales, group)
+        load_rows(2)
+        load_rows(3)
+        load_scales(w2_scales, W2_scales, 0)
         load_w2(0)
-        load_norm(0)
+        load_norm(b2_rows, b2)
         load_w1(1)
+        load_norm(gamma_rows, gamma)
+        load_norm(beta_rows, beta)
+        load_scales(w1_scales, W1_scales, 1)
+        for group in range(1, NC * H_PASSES // PLANES):
+            load_scales(w2_scales, W2_scales, group)
+
+        def stream_weights(e):
+            if e < NC:
+                load_w2(e)
+            if e + 1 < NC:
+                load_w1(e + 1)
 
         live = {
             name: {}
@@ -110,21 +120,14 @@ def tile_patchwork_e_kernel(
             )
         }
 
-        def stream_weights(e):
-            if 0 < e < NC:
-                load_w2(e)
-                load_norm(e)
-            if e + 1 < NC:
-                load_w1(e + 1)
-
         def turn_b1():
             words = b1_rows[:].bitcast(F32)
-            b1_t = psum.tile([P, 2, P], F32, name="x_t")
+            b1_t = psum.tile([P, 2, 2, P], F32, name="x_t")
             for u in range(2):
-                nc.tensor.transpose(b1_t[:, u, :], words[:, u::2], identity[:])
+                nc.tensor.transpose(b1_t[:, 0, u, :], words[:, u::2], identity[:])
             nc.vector.tensor_copy(
                 out=b1_cols[:].rearrange("q r (u c) -> q r u c", c=2),
-                in_=b1_t[:].rearrange("q u r -> q (u r)").bitcast(BF16).rearrange(
+                in_=b1_t[:, 0].rearrange("q u r -> q (u r)").bitcast(BF16).rearrange(
                     "q (u r c) -> q r u c", u=2, c=2
                 )[:, : NC * H_PASSES],
             )
@@ -135,124 +138,133 @@ def tile_patchwork_e_kernel(
                 in_=w1_scales[:, group, :].rearrange("p (g q t) -> p g t q", t=PACK, q=P),
             )
 
-        def sort_w1(e):
-            w1 = work.tile([P, H], U32, align_bytes=64, bufs=2)
-            nc.gpsimd.tensor_copy(
-                out=w1[:].bitcast(I32).rearrange("p (g t q) -> p g t q", t=PACK, q=P),
-                in_=w1_words[:, e, :].bitcast(I32).rearrange("p (g q t) -> p g t q", t=PACK, q=P),
+        def sort_w1(e, g):
+            if g == 0:
+                live["w1"][e] = work.tile([P, H], U32, align_bytes=64, bufs=2, name="w1_sorted")
+            half = slice(g * 512, (g + 1) * 512)
+            nc.vector.tensor_copy(
+                out=live["w1"][e][:, half].bitcast(I32).rearrange("p (t q) -> p t q", t=PACK),
+                in_=w1_words[:, e, half].bitcast(I32).rearrange("p (q t) -> p t q", t=PACK),
             )
-            live["w1"][e] = w1
 
-        def sort_x(n):
-            e, r = divmod(n, ROW_TILES)
-            x_sorted = work.tile([P, APC], BF16, bufs=4)
-            nc.gpsimd.tensor_scalar(
-                out=x_sorted[:].rearrange("b (u q c) -> b u q c", u=2, c=2),
-                in0=tri_sb[:, r, :].rearrange("b (q u c e) -> b e u q c", u=2, c=2, e=NC)[:, e],
-                scalar1=1.0,
-                scalar2=0.0,
-                op0=ALU.mult,
-                op1=ALU.add,
-            )
-            live["x_sorted"][n] = x_sorted
+        def sort_x(m):
+            e, half = divmod(m, 2)
+            x_sorted = work.tile([P, 2, APC], BF16)
+            for k in range(2):
+                view = x_sorted[:, k, :].rearrange("b (u q c) -> b u q c", u=2, c=2)
+                source = tri_sb[:, 2 * half + k, :].rearrange("b (q u c e) -> b e u q c", u=2, c=2, e=NC)[:, e]
+                if m == 0 and k == 1:
+                    nc.vector.tensor_copy(out=view, in_=source)
+                else:
+                    nc.gpsimd.tensor_scalar(out=view, in0=source, scalar1=1.0, scalar2=0.0, op0=ALU.mult, op1=ALU.add)
+            live["x_sorted"][m] = x_sorted
 
-        def transpose_x(n):
-            words = live["x_sorted"][n][:].bitcast(F32)
-            x_t = psum.tile([P, 2, P], F32)
-            for u in range(2):
-                nc.tensor.transpose(x_t[:, u, :], words[:, u * P : (u + 1) * P], identity[:])
-            live["x_t"][n] = x_t
+        def transpose_x(m):
+            x_t = psum.tile([P, 2, 2, P], F32)
+            for k in range(2):
+                words = live["x_sorted"][m][:, k, :].bitcast(F32)
+                for u in range(2):
+                    nc.tensor.transpose(x_t[:, k, u, :], words[:, u * P : (u + 1) * P], identity[:])
+            live["x_t"][m] = x_t
 
-        def group_x(n):
-            x_grouped = work.tile([P, P * PACK], BF16, align_bytes=64)
+        def group_x(m):
+            x_grouped = work.tile([P, 2 * P * PACK], BF16, align_bytes=64, bufs=2)
             nc.scalar.copy(
-                out=x_grouped[:].bitcast(F32).rearrange("q (b u) -> q b u", u=2),
-                in_=live["x_t"][n][:].rearrange("q u b -> q b u"),
+                out=x_grouped[:].bitcast(F32).rearrange("q (k b u) -> q k b u", k=2, u=2),
+                in_=live["x_t"][m][:].rearrange("q k u b -> q k b u"),
             )
-            live["x_grouped"][n] = x_grouped
+            live["x_grouped"][m] = x_grouped
 
-        def quantise_x(n):
-            e, r = divmod(n, ROW_TILES)
-            if r == 0:
-                x_codes = work.tile([P, B], U32, align_bytes=64)
-                x_scales = work.tile([P, B], U8, align_bytes=64)
-                live["x_codes"][e] = x_codes
-                live["x_scales"][e] = x_scales
-            rows = slice(r * P, (r + 1) * P)
+        def quantise_x(m):
+            e, half = divmod(m, 2)
+            if half == 0:
+                live["x_codes"][e] = work.tile([P, B], U32, align_bytes=64, name="x_codes")
+                live["x_scales"][e] = work.tile([P, B], U8, align_bytes=64, name="x_scales")
+            rows = half_rows(half)
             nc.vector.quantize_mx(
                 out=live["x_codes"][e][:, rows].bitcast(FP8X4),
                 scales=live["x_scales"][e][:, rows],
-                in_=live["x_grouped"][n][:],
+                in_=live["x_grouped"][m][:],
+            )
+
+        def half_rows(half):
+            return slice(half * 2 * P, (half + 1) * 2 * P)
+
+        def by_halves(e):
+            return e == 0 or e == NC - 1
+
+        def part(n):
+            e, i = divmod(n, ROW_TILES)
+            major, minor = divmod(i, 2)
+            return (minor, major) if by_halves(e) else (major, minor)
+
+        def mx(e, j, rows, z):
+            group, plane = divmod(e, PLANES)
+            cols = slice(j * P, (j + 1) * P)
+            nc.tensor.matmul_mx(
+                out=z,
+                lhsT=live["w1"][e][:, cols].bitcast(FP8X4),
+                lhsT_scale=w1_scales_sorted[4 * plane : P, group, cols],
+                rhs=live["x_codes"][e][:, rows].bitcast(FP8X4),
+                rhs_scale=live["x_scales"][e][:, rows],
+                start=True,
+                stop=True,
             )
 
         def first_matmul(n):
-            e, i = divmod(n, ROW_TILES)
-            group, plane = divmod(e, PLANES)
-            x_codes = live["x_codes"][e]
-            x_scales = live["x_scales"][e]
-            pair = []
-            for j in (2 * i, 2 * i + 1):
-                cols = slice(j * P, (j + 1) * P)
+            e = n // ROW_TILES
+            g, half = part(n)
+            banks = []
+            for k in range(2):
                 z = psum.tile([P, B], F32, bufs=4)
-                nc.tensor.matmul_mx(
-                    out=z[:],
-                    lhsT=live["w1"][e][:, cols].bitcast(FP8X4),
-                    lhsT_scale=w1_scales_sorted[4 * plane : P, group, cols],
-                    rhs=x_codes[:].bitcast(FP8X4),
-                    rhs_scale=x_scales[:],
-                    start=True,
-                    stop=True,
-                )
-                pair.append(z)
-            live["z"][n] = pair
+                if by_halves(e):
+                    for c in range(2):
+                        mx(e, PACK * g + 2 * k + c, half_rows(half), z[:, half_rows(c)])
+                else:
+                    mx(e, PACK * g + 2 * half + k, slice(0, B), z[:])
+                banks.append(z)
+            live["z"][n] = banks
 
-        def relu_on_vector(n):
-            e, i = divmod(n, ROW_TILES)
-            g, half = divmod(i, 2)
-            if half == 0:
-                r = work.tile([P, PACK, B], F32)
-                live["r"][n // 2] = r
-            t = 2 * half
-            nc.vector.tensor_scalar(
-                out=live["r"][n // 2][:, t, :],
-                in0=live["z"][n][0][:],
-                scalar1=b1_cols[:, e * H_PASSES + g, t : t + 1],
-                scalar2=0.0,
-                op0=ALU.add,
-                op1=ALU.max,
-            )
-
-        def relu_on_scalar(n):
-            e, i = divmod(n, ROW_TILES)
-            g, half = divmod(i, 2)
-            t = 2 * half + 1
-            nc.scalar.activation(
-                out=live["r"][n // 2][:, t, :],
-                in_=live["z"][n][1][:],
-                func=ACT.Relu,
-                bias=b1_cols[:, e * H_PASSES + g, t : t + 1],
-            )
+        def relu(n, k):
+            e = n // ROW_TILES
+            g, half = part(n)
+            key = (e, g, half) if by_halves(e) else (e, g)
+            if key not in live["r"]:
+                live["r"][key] = work.tile([P, PACK, B], F32, name="r")
+            r = live["r"][key]
+            z = live["z"][n][k]
+            if by_halves(e):
+                jobs = [(2 * k + c, half_rows(half), z[:, half_rows(c)]) for c in range(2)]
+            else:
+                jobs = [(2 * half + k, slice(0, B), z[:])]
+            for t, rows, source in jobs:
+                bias = b1_cols[:, e * H_PASSES + g, t : t + 1]
+                if k == 0 and n % 2 == 0:
+                    nc.vector.tensor_scalar(
+                        out=r[:, t, rows], in0=source, scalar1=bias, scalar2=0.0, op0=ALU.add, op1=ALU.max
+                    )
+                else:
+                    nc.scalar.activation(out=r[:, t, rows], in_=source, func=ACT.Relu, bias=bias)
 
         def square(n):
-            half = n % 2
-            rows = slice(half * 2 * P, (half + 1) * 2 * P)
+            e = n // ROW_TILES
+            g, half = part(n)
+            key = (e, g, half) if by_halves(e) else (e, g)
             h_grouped = work.tile([P, 2 * P, PACK], BF16, align_bytes=64)
             nc.scalar.activation(
-                out=h_grouped[:],
-                in_=live["r"][n // 2][:, :, rows].rearrange("q t b -> q b t"),
+                out=h_grouped[:].rearrange("q (c i) t -> q c t i", i=4),
+                in_=live["r"][key][:, :, half_rows(half)].rearrange("q t (c i) -> q c t i", i=4),
                 func=ACT.Square,
             )
             live["h_grouped"][n] = h_grouped
 
         def quantise_h(n):
             e, i = divmod(n, ROW_TILES)
-            g, half = divmod(i, 2)
+            g, half = part(n)
             if i == 0:
-                h_codes = work.tile([P, H_PASSES, B], U32, align_bytes=64)
-                h_scales = work.tile([P, H_PASSES, B], U8, align_bytes=64)
-                live["h_codes"][e] = h_codes
-                live["h_scales"][e] = h_scales
-            rows = slice(half * 2 * P, (half + 1) * 2 * P)
+                live["h_codes"][e] = work.tile([P, H_PASSES, B], U32, align_bytes=64, name="h_codes")
+                live["h_scales"][e] = work.tile([P, H_PASSES, B], U8, align_bytes=64, name="h_scales")
+            rows = half_rows(half)
             nc.vector.quantize_mx(
                 out=live["h_codes"][e][:, g, rows].bitcast(FP8X4),
                 scales=live["h_scales"][e][:, g, rows],
@@ -293,7 +305,7 @@ def tile_patchwork_e_kernel(
             live["t_sum"][n] = t_sum
 
         def mean(n):
-            neg_mean = work.tile([P, 1], F32)
+            neg_mean = work.tile([P, 1], F32, bufs=4)
             nc.gpsimd.tensor_scalar(
                 out=neg_mean[:],
                 in0=live["t_sum"][n][:],
@@ -305,23 +317,24 @@ def tile_patchwork_e_kernel(
             live["neg_mean"][n] = neg_mean
 
         def squares(n):
+            if n % 2 == 0:
+                live["sq_sum"][n // 2] = work.tile([P, 2], F32, name="sq_sum")
             squared = work.tile([P, D], BF16)
-            sq_sum = work.tile([P, 1], F32)
             nc.scalar.activation(
                 out=squared[:],
                 in_=live["t"][n][:],
                 func=ACT.Square,
                 bias=live["neg_mean"][n][:],
-                accum_out=sq_sum[:],
+                accum_out=live["sq_sum"][n // 2][:, n % 2 : n % 2 + 1],
             )
-            live["sq_sum"][n] = sq_sum
 
         def inverse_deviation(n):
-            rstd = work.tile([P, 1], F32)
-            nc.scalar.activation(
-                out=rstd[:], in_=live["sq_sum"][n][:], func=ACT.Abs_reciprocal_sqrt, scale=1.0 / D, bias=eps[:]
-            )
-            live["rstd"][n] = rstd
+            if n % 2 == 1:
+                rstd = work.tile([P, 2], F32)
+                nc.scalar.activation(
+                    out=rstd[:], in_=live["sq_sum"][n // 2][:], func=ACT.Abs_reciprocal_sqrt, scale=1.0 / D, bias=eps[:]
+                )
+                live["rstd"][n // 2] = rstd
 
         def centre_times_gamma(n):
             e = n // ROW_TILES
@@ -341,40 +354,74 @@ def tile_patchwork_e_kernel(
             nc.vector.scalar_tensor_tensor(
                 out=t[:],
                 in0=t[:],
-                scalar=live["rstd"][n][:],
+                scalar=live["rstd"][n // 2][:, n % 2 : n % 2 + 1],
                 in1=beta_rows[:, e, :],
                 op0=ALU.mult,
                 op1=ALU.add,
             )
             nc.sync.dma_start(out=out[r * P : (r + 1) * P, e * D : (e + 1) * D], in_=t[:])
 
-        def run(stage, n):
-            if 0 <= n < ITEMS:
-                stage(n)
+        def at(lag_normal, lag_halves):
+            steps = {}
+            for n in range(ITEMS):
+                lag = lag_halves if by_halves(n // ROW_TILES) else lag_normal
+                steps.setdefault(n + lag, []).append(n)
+            return steps
+
+        relu_at = at(1, 1)
+        square_at = at(3, 2)
+        quantise_h_at = at(4, 3)
+        second_at = at(7, 5)
+        add_at = at(8, 6)
+        squares_at = at(9, 7)
+        centre_at = at(9, 7)
+        scale_at = at(11, 9)
+
+        turn_at = {-2: [0], -1: [2], 2: [3]}
+        for m in range(4, 2 * NC):
+            turn_at[2 * m - 5] = [m]
+
+        def run(stage, items, *more):
+            for n in items:
+                if 0 <= n:
+                    stage(n, *more)
 
         turn_b1()
         sort_w1_scales(0)
-        for step in range(-8, ITEMS + 11):
+        sort_x(0)
+        sort_w1(0, 0)
+        sort_w1(0, 1)
+        sort_x(2)
+        sort_x(1)
+        sort_x(3)
+        for step in range(-2, ITEMS + 11):
             if step >= 0 and step % ROW_TILES == 0:
                 stream_weights(step // ROW_TILES + 1)
-            run(sort_x, step + 8)
-            run(relu_on_vector, step - 1)
-            run(relu_on_scalar, step - 1)
-            run(squares, step - 9)
-            run(transpose_x, step + 6)
-            run(second_matmul, step - 7)
-            run(first_matmul, step)
-            run(square, step - 3)
-            run(inverse_deviation, step - 9)
-            run(group_x, step + 6)
-            run(add_b2, step - 8)
-            run(quantise_h, step - 4)
-            run(quantise_x, step + 5)
-            run(mean, step - 8)
-            run(scale_plus_beta, step - 10)
-            run(centre_times_gamma, step - 9)
-            ahead, i = divmod(step + 2, ROW_TILES)
-            if i == 0 and 0 <= ahead < NC:
-                sort_w1(ahead)
+            run(sort_x, turn_at.get(step + 2, []) if step + 2 > 2 else [])
+            run(relu, relu_at.get(step, []), 0)
+            run(relu, relu_at.get(step, []), 1)
+            run(squares, squares_at.get(step, []))
             if step == 2:
+                run(square, square_at.get(step, []))
+                transpose_x(1)
+                group_x(1)
+                quantise_x(1)
+            run(transpose_x, turn_at.get(step, []))
+            run(second_matmul, second_at.get(step, []))
+            if 0 <= step < ITEMS:
+                first_matmul(step)
+            if step != 2:
+                run(square, square_at.get(step, []))
+            run(inverse_deviation, squares_at.get(step, []))
+            run(group_x, turn_at.get(step, []))
+            run(add_b2, add_at.get(step, []))
+            run(quantise_h, quantise_h_at.get(step, []))
+            run(quantise_x, turn_at.get(step - 1, []))
+            run(mean, add_at.get(step, []))
+            run(scale_plus_beta, scale_at.get(step, []))
+            run(centre_times_gamma, centre_at.get(step, []))
+            ahead, i = divmod(step + 3, ROW_TILES)
+            if 0 < ahead < NC and i < 2:
+                sort_w1(ahead, i)
+            if step == 4:
                 sort_w1_scales(1)

@@ -45,18 +45,19 @@ def tile_patchwork_e_kernel(
         w2_scales = keep.tile([P, NC * H_PASSES // PLANES, D], U8, align_bytes=64)
         b1_rows = keep.tile([P, H // H_PASSES], BF16)
         b1_cols = keep.tile([P, NC * H_PASSES, PACK], F32)
-        b2_rows = keep.tile([P, NC, D], BF16)
-        gamma_rows = keep.tile([P, NC, D], BF16)
-        beta_rows = keep.tile([P, NC, D], BF16)
+        norm_rows = keep.tile([P, 3, D], BF16)
         identity = keep.tile([P, P], F32)
+        identity_bf = keep.tile([P, P], BF16)
         eps = keep.tile([P, 1], F32)
         table_warm = keep.tile([P, 1], F32)
 
         nc.vector.memset(b1_rows[:], 0.0)
+        nc.vector.memset(norm_rows[:], 0.0)
         nc.vector.memset(w1_scales[:].bitcast(I32), 0)
         nc.vector.memset(w2_scales[:].bitcast(I32), 0)
         nc.vector.memset(eps[:], LN_EPS)
         make_identity(nc, identity[:])
+        make_identity(nc, identity_bf[:])
         nc.scalar.activation(out=table_warm[:], in_=eps[:], func=ACT.Abs_reciprocal_sqrt)
 
         def load_rows(r):
@@ -82,26 +83,21 @@ def tile_patchwork_e_kernel(
                 in_=W2_words[passes].rearrange("g p n t -> p g (n t)").bitcast(I32),
             )
 
-        def load_norm(rows, param):
-            nc.sync.dma_start(
-                out=rows[:].rearrange("p e n -> p (e n)"), in_=param.rearrange("e n -> (e n)").partition_broadcast(P)
-            )
 
-        load_rows(0)
-        load_rows(1)
         nc.sync.dma_start(
             out=b1_rows[: NC * H_PASSES, :], in_=b1.rearrange("e (g c) -> (e g) c", g=H_PASSES)
         )
+        load_rows(0)
+        load_rows(1)
         load_scales(w1_scales, W1_scales, 0)
         load_w1(0)
         load_rows(2)
         load_rows(3)
         load_scales(w2_scales, W2_scales, 0)
+        for k, param in enumerate((b2, gamma, beta)):
+            nc.sync.dma_start(out=norm_rows[:NC, k, :], in_=param)
         load_w2(0)
-        load_norm(b2_rows, b2)
         load_w1(1)
-        load_norm(gamma_rows, gamma)
-        load_norm(beta_rows, beta)
         load_scales(w1_scales, W1_scales, 1)
         for group in range(1, NC * H_PASSES // PLANES):
             load_scales(w2_scales, W2_scales, group)
@@ -115,7 +111,7 @@ def tile_patchwork_e_kernel(
         live = {
             name: {}
             for name in (
-                "w1", "x_sorted", "x_t", "x_grouped", "x_codes", "x_scales", "z", "r", "h_grouped",
+                "w1", "b2", "norm", "x_sorted", "x_t", "x_grouped", "x_codes", "x_scales", "z", "r", "h_grouped",
                 "h_codes", "h_scales", "y", "t", "t_sum", "neg_mean", "sq_sum", "rstd",
             )
         }
@@ -146,6 +142,28 @@ def tile_patchwork_e_kernel(
                 out=live["w1"][e][:, half].bitcast(I32).rearrange("p (t q) -> p t q", t=PACK),
                 in_=w1_words[:, e, half].bitcast(I32).rearrange("p (q t) -> p t q", t=PACK),
             )
+
+        def spread(e, k, row):
+            nc.tensor.matmul(
+                row,
+                lhsT=identity_bf[:, e : e + 1].to_broadcast([P, P]),
+                rhs=norm_rows[:, k, :],
+                start=True,
+                stop=True,
+            )
+
+        def spread_b2(e):
+            b2_t = psum.tile([P, 2, D], BF16, name="x_t")
+            spread(e, 0, b2_t[:, 0, :])
+            b2_row = work.tile([P, D], BF16)
+            nc.scalar.copy(out=b2_row[:], in_=b2_t[:, 0, :])
+            live["b2"][e] = b2_row
+
+        def spread_norm(e):
+            norm = psum.tile([P, 2, D], BF16, bufs=2)
+            for k in range(2):
+                spread(e, 1 + k, norm[:, k, :])
+            live["norm"][e] = norm
 
         def sort_x(m):
             e, half = divmod(m, 2)
@@ -216,7 +234,7 @@ def tile_patchwork_e_kernel(
             g, half = part(n)
             banks = []
             for k in range(2):
-                z = psum.tile([P, B], F32, bufs=4)
+                z = psum.tile([P, B], F32, bufs=3)
                 if by_halves(e):
                     for c in range(2):
                         mx(e, PACK * g + 2 * k + c, half_rows(half), z[:, half_rows(c)])
@@ -274,7 +292,7 @@ def tile_patchwork_e_kernel(
         def second_matmul(n):
             e, r = divmod(n, ROW_TILES)
             rows = slice(r * P, (r + 1) * P)
-            y = psum.tile([P, D], F32, bufs=3)
+            y = psum.tile([P, D], F32, bufs=2)
             for g in range(H_PASSES):
                 group, plane = divmod(e * H_PASSES + g, PLANES)
                 nc.tensor.matmul_mx(
@@ -296,7 +314,7 @@ def tile_patchwork_e_kernel(
                 out=t[:],
                 in0=live["y"][n][:],
                 scalar=1.0,
-                in1=b2_rows[:, e, :],
+                in1=live["b2"][e][:],
                 op0=ALU.mult,
                 op1=ALU.add,
                 accum_out=t_sum[:],
@@ -343,7 +361,7 @@ def tile_patchwork_e_kernel(
                 out=t[:],
                 in0=t[:],
                 scalar=live["neg_mean"][n][:],
-                in1=gamma_rows[:, e, :],
+                in1=live["norm"][e][:, 0, :],
                 op0=ALU.add,
                 op1=ALU.mult,
             )
@@ -355,7 +373,7 @@ def tile_patchwork_e_kernel(
                 out=t[:],
                 in0=t[:],
                 scalar=live["rstd"][n // 2][:, n % 2 : n % 2 + 1],
-                in1=beta_rows[:, e, :],
+                in1=live["norm"][e][:, 1, :],
                 op0=ALU.mult,
                 op1=ALU.add,
             )
@@ -406,6 +424,14 @@ def tile_patchwork_e_kernel(
                 transpose_x(1)
                 group_x(1)
                 quantise_x(1)
+            if step == 3:
+                spread_b2(0)
+                spread_norm(0)
+            comp, i = divmod(step - 7, ROW_TILES)
+            if i == 0 and 0 < comp < NC:
+                spread_norm(comp)
+            if i == 3 and 0 <= comp < NC - 1:
+                spread_b2(comp + 1)
             run(transpose_x, turn_at.get(step, []))
             run(second_matmul, second_at.get(step, []))
             if 0 <= step < ITEMS:

@@ -52,10 +52,10 @@ def tile_patchwork_e_kernel(
         table_warm = keep.tile([P, 1], F32)
 
         nc.vector.memset(b1_rows[:], 0.0)
-        nc.vector.memset(norm_rows[:], 0.0)
+        nc.vector.memset(eps[:], LN_EPS)
         nc.vector.memset(w1_scales[:].bitcast(I32), 0)
         nc.vector.memset(w2_scales[:].bitcast(I32), 0)
-        nc.vector.memset(eps[:], LN_EPS)
+        nc.vector.memset(norm_rows[:].bitcast(I32), 0)
         make_identity(nc, identity[:])
         make_identity(nc, identity_bf[:])
         nc.scalar.activation(out=table_warm[:], in_=eps[:], func=ACT.Abs_reciprocal_sqrt)
@@ -93,11 +93,11 @@ def tile_patchwork_e_kernel(
         load_w1(0)
         load_rows(2)
         load_rows(3)
+        load_w1(1)
         load_scales(w2_scales, W2_scales, 0)
         for k, param in enumerate((b2, gamma, beta)):
             nc.sync.dma_start(out=norm_rows[:NC, k, :], in_=param)
         load_w2(0)
-        load_w1(1)
         load_scales(w1_scales, W1_scales, 1)
         for group in range(1, NC * H_PASSES // PLANES):
             load_scales(w2_scales, W2_scales, group)
@@ -257,7 +257,7 @@ def tile_patchwork_e_kernel(
                 jobs = [(2 * half + k, slice(0, B), z[:])]
             for t, rows, source in jobs:
                 bias = b1_cols[:, e * H_PASSES + g, t : t + 1]
-                if k == 0 and n % 2 == 0:
+                if k == 0 and n % 4 == 0 and e < NC - 1:
                     nc.vector.tensor_scalar(
                         out=r[:, t, rows], in0=source, scalar1=bias, scalar2=0.0, op0=ALU.add, op1=ALU.max
                     )
@@ -269,11 +269,15 @@ def tile_patchwork_e_kernel(
             g, half = part(n)
             key = (e, g, half) if by_halves(e) else (e, g)
             h_grouped = work.tile([P, 2 * P, PACK], BF16, align_bytes=64)
-            nc.scalar.activation(
-                out=h_grouped[:].rearrange("q (c i) t -> q c t i", i=4),
-                in_=live["r"][key][:, :, half_rows(half)].rearrange("q t (c i) -> q c t i", i=4),
-                func=ACT.Square,
-            )
+            r = live["r"][key]
+            for k in range(2):
+                rows = slice((2 * half + k) * P, (2 * half + k + 1) * P)
+                source = r[:, :, rows].rearrange("q t (c i) -> q c t i", i=4)
+                target = h_grouped[:, k * P : (k + 1) * P, :].rearrange("q (c i) t -> q c t i", i=4)
+                if k == 0:
+                    nc.scalar.activation(out=target, in_=source, func=ACT.Square)
+                else:
+                    nc.gpsimd.tensor_tensor(out=target, in0=source, in1=source, op=ALU.mult)
             live["h_grouped"][n] = h_grouped
 
         def quantise_h(n):
@@ -308,7 +312,7 @@ def tile_patchwork_e_kernel(
 
         def add_b2(n):
             e = n // ROW_TILES
-            t = work.tile([P, D], F32, bufs=8)
+            t = work.tile([P, D], F32, bufs=10)
             t_sum = work.tile([P, 1], F32)
             nc.vector.scalar_tensor_tensor(
                 out=t[:],
@@ -323,15 +327,8 @@ def tile_patchwork_e_kernel(
             live["t_sum"][n] = t_sum
 
         def mean(n):
-            neg_mean = work.tile([P, 1], F32, bufs=4)
-            nc.gpsimd.tensor_scalar(
-                out=neg_mean[:],
-                in0=live["t_sum"][n][:],
-                scalar1=-1.0 / D,
-                scalar2=0.0,
-                op0=ALU.mult,
-                op1=ALU.add,
-            )
+            neg_mean = work.tile([P, 1], F32, bufs=6)
+            nc.scalar.mul(neg_mean[:], live["t_sum"][n][:], -1.0 / D)
             live["neg_mean"][n] = neg_mean
 
         def squares(n):
@@ -388,12 +385,13 @@ def tile_patchwork_e_kernel(
 
         relu_at = at(1, 1)
         square_at = at(3, 2)
-        quantise_h_at = at(4, 3)
-        second_at = at(7, 5)
-        add_at = at(8, 6)
-        squares_at = at(9, 7)
-        centre_at = at(9, 7)
-        scale_at = at(11, 9)
+        quantise_h_at = at(5, 4)
+        second_at = at(8, 6)
+        add_at = at(9, 7)
+        mean_at = at(10, 8)
+        squares_at = at(11, 9)
+        centre_at = at(11, 9)
+        scale_at = at(13, 11)
 
         turn_at = {-2: [0], -1: [2], 2: [3]}
         for m in range(4, 2 * NC):
@@ -405,16 +403,17 @@ def tile_patchwork_e_kernel(
                     stage(n, *more)
 
         turn_b1()
-        sort_w1_scales(0)
         sort_x(0)
+        sort_w1_scales(0)
         sort_w1(0, 0)
         sort_w1(0, 1)
         sort_x(2)
         sort_x(1)
         sort_x(3)
-        for step in range(-2, ITEMS + 11):
+        for step in range(-2, ITEMS + 13):
             if step >= 0 and step % ROW_TILES == 0:
                 stream_weights(step // ROW_TILES + 1)
+            run(mean, mean_at.get(step, []))
             run(sort_x, turn_at.get(step + 2, []) if step + 2 > 2 else [])
             run(relu, relu_at.get(step, []), 0)
             run(relu, relu_at.get(step, []), 1)
@@ -427,10 +426,10 @@ def tile_patchwork_e_kernel(
             if step == 3:
                 spread_b2(0)
                 spread_norm(0)
-            comp, i = divmod(step - 7, ROW_TILES)
+            comp, i = divmod(step - 9, ROW_TILES)
             if i == 0 and 0 < comp < NC:
                 spread_norm(comp)
-            if i == 3 and 0 <= comp < NC - 1:
+            if i == 1 and 0 <= comp < NC - 1:
                 spread_b2(comp + 1)
             run(transpose_x, turn_at.get(step, []))
             run(second_matmul, second_at.get(step, []))
@@ -443,10 +442,9 @@ def tile_patchwork_e_kernel(
             run(add_b2, add_at.get(step, []))
             run(quantise_h, quantise_h_at.get(step, []))
             run(quantise_x, turn_at.get(step - 1, []))
-            run(mean, add_at.get(step, []))
             run(scale_plus_beta, scale_at.get(step, []))
             run(centre_times_gamma, centre_at.get(step, []))
-            ahead, i = divmod(step + 3, ROW_TILES)
+            ahead, i = divmod(step + 2, ROW_TILES)
             if 0 < ahead < NC and i < 2:
                 sort_w1(ahead, i)
             if step == 4:

@@ -91,9 +91,9 @@ def tile_patchwork_e_kernel(
         load_rows(1)
         load_scales(w1_scales, W1_scales, 0)
         load_w1(0)
+        load_w1(1)
         load_rows(2)
         load_rows(3)
-        load_w1(1)
         load_scales(w2_scales, W2_scales, 0)
         for k, param in enumerate((b2, gamma, beta)):
             nc.sync.dma_start(out=norm_rows[:NC, k, :], in_=param)
@@ -136,7 +136,7 @@ def tile_patchwork_e_kernel(
 
         def sort_w1(e, g):
             if g == 0:
-                live["w1"][e] = work.tile([P, H], U32, align_bytes=64, bufs=2, name="w1_sorted")
+                live["w1"][e] = work.tile([P, H], U32, align_bytes=64, bufs=3, name="w1_sorted")
             half = slice(g * 512, (g + 1) * 512)
             nc.vector.tensor_copy(
                 out=live["w1"][e][:, half].bitcast(I32).rearrange("p (t q) -> p t q", t=PACK),
@@ -209,7 +209,7 @@ def tile_patchwork_e_kernel(
             return slice(half * 2 * P, (half + 1) * 2 * P)
 
         def by_halves(e):
-            return e == 0 or e == NC - 1
+            return e < 2 or e == NC - 1
 
         def part(n):
             e, i = divmod(n, ROW_TILES)
@@ -257,7 +257,7 @@ def tile_patchwork_e_kernel(
                 jobs = [(2 * half + k, slice(0, B), z[:])]
             for t, rows, source in jobs:
                 bias = b1_cols[:, e * H_PASSES + g, t : t + 1]
-                if k == 0 and n % 4 == 0 and e < NC - 1:
+                if k == 0 and (n % 4 != 3 or n < 8):
                     nc.vector.tensor_scalar(
                         out=r[:, t, rows], in0=source, scalar1=bias, scalar2=0.0, op0=ALU.add, op1=ALU.max
                     )
@@ -270,14 +270,9 @@ def tile_patchwork_e_kernel(
             key = (e, g, half) if by_halves(e) else (e, g)
             h_grouped = work.tile([P, 2 * P, PACK], BF16, align_bytes=64)
             r = live["r"][key]
-            for k in range(2):
-                rows = slice((2 * half + k) * P, (2 * half + k + 1) * P)
-                source = r[:, :, rows].rearrange("q t (c i) -> q c t i", i=4)
-                target = h_grouped[:, k * P : (k + 1) * P, :].rearrange("q (c i) t -> q c t i", i=4)
-                if k == 0:
-                    nc.scalar.activation(out=target, in_=source, func=ACT.Square)
-                else:
-                    nc.gpsimd.tensor_tensor(out=target, in0=source, in1=source, op=ALU.mult)
+            source = r[:, :, half_rows(half)].rearrange("q t (c i) -> q c t i", i=4)
+            target = h_grouped[:].rearrange("q (c i) t -> q c t i", i=4)
+            nc.scalar.activation(out=target, in_=source, func=ACT.Square)
             live["h_grouped"][n] = h_grouped
 
         def quantise_h(n):
@@ -376,26 +371,31 @@ def tile_patchwork_e_kernel(
             )
             nc.sync.dma_start(out=out[r * P : (r + 1) * P, e * D : (e + 1) * D], in_=t[:])
 
+        order = [0, 1, 4, 5, 2, 3, 6, 7] + list(range(2 * ROW_TILES, ITEMS))
+
         def at(lag_normal, lag_halves):
             steps = {}
-            for n in range(ITEMS):
+            for place, n in enumerate(order):
                 lag = lag_halves if by_halves(n // ROW_TILES) else lag_normal
-                steps.setdefault(n + lag, []).append(n)
+                steps.setdefault(place + lag, []).append(n)
             return steps
 
-        relu_at = at(1, 1)
-        square_at = at(3, 2)
-        quantise_h_at = at(5, 4)
-        second_at = at(8, 6)
-        add_at = at(9, 7)
-        mean_at = at(10, 8)
-        squares_at = at(11, 9)
-        centre_at = at(11, 9)
-        scale_at = at(13, 11)
+        multiply_at = at(0, 0)
 
-        turn_at = {-2: [0], -1: [2], 2: [3]}
-        for m in range(4, 2 * NC):
-            turn_at[2 * m - 5] = [m]
+        relu_at = at(1, 1)
+        square_at = at(3,2)
+        quantise_h_at = at(4,3)
+        second_at = at(7,5)
+        add_at = at(7,6)
+        mean_at = at(8,7)
+        squares_at = at(8,7)
+        centre_at = at(9,8)
+        scale_at = at(10,9)
+
+        turn_at = {-2: [0], -1: [2], 2: [1], 4: [3]}
+        for e in range(2, NC):
+            turn_at[ROW_TILES * e - 3] = [2 * e]
+            turn_at[ROW_TILES * e - 2] = [2 * e + 1]
 
         def run(stage, items, *more):
             for n in items:
@@ -408,35 +408,24 @@ def tile_patchwork_e_kernel(
         sort_w1(0, 0)
         sort_w1(0, 1)
         sort_x(2)
-        sort_x(1)
-        sort_x(3)
         for step in range(-2, ITEMS + 13):
             if step >= 0 and step % ROW_TILES == 0:
                 stream_weights(step // ROW_TILES + 1)
             run(mean, mean_at.get(step, []))
-            run(sort_x, turn_at.get(step + 2, []) if step + 2 > 2 else [])
+            run(sort_x, turn_at.get(step + 2, []) if step >= 0 else [])
             run(relu, relu_at.get(step, []), 0)
             run(relu, relu_at.get(step, []), 1)
             run(squares, squares_at.get(step, []))
-            if step == 2:
-                run(square, square_at.get(step, []))
-                transpose_x(1)
-                group_x(1)
-                quantise_x(1)
-            if step == 3:
-                spread_b2(0)
-                spread_norm(0)
-            comp, i = divmod(step - 9, ROW_TILES)
-            if i == 0 and 0 < comp < NC:
-                spread_norm(comp)
-            if i == 1 and 0 <= comp < NC - 1:
-                spread_b2(comp + 1)
-            run(transpose_x, turn_at.get(step, []))
+            for n in add_at.get(step + 1, []):
+                if n % ROW_TILES == 0:
+                    spread_b2(n // ROW_TILES)
+            for n in centre_at.get(step, []):
+                if n % ROW_TILES == 0:
+                    spread_norm(n // ROW_TILES)
             run(second_matmul, second_at.get(step, []))
-            if 0 <= step < ITEMS:
-                first_matmul(step)
-            if step != 2:
-                run(square, square_at.get(step, []))
+            run(first_matmul, multiply_at.get(step, []))
+            run(transpose_x, turn_at.get(step, []))
+            run(square, square_at.get(step, []))
             run(inverse_deviation, squares_at.get(step, []))
             run(group_x, turn_at.get(step, []))
             run(add_b2, add_at.get(step, []))
@@ -444,8 +433,10 @@ def tile_patchwork_e_kernel(
             run(quantise_x, turn_at.get(step - 1, []))
             run(scale_plus_beta, scale_at.get(step, []))
             run(centre_times_gamma, centre_at.get(step, []))
+            if step in (0, 1):
+                sort_w1(1, step)
             ahead, i = divmod(step + 2, ROW_TILES)
-            if 0 < ahead < NC and i < 2:
+            if 1 < ahead < NC and i < 2:
                 sort_w1(ahead, i)
             if step == 4:
                 sort_w1_scales(1)

@@ -105,6 +105,7 @@ def tile_patchwork_e_kernel(
         def stream_weights(e):
             if e < NC:
                 load_w2(e)
+                load_b2(e)
             if e + 1 < NC:
                 load_w1(e + 1)
 
@@ -134,13 +135,11 @@ def tile_patchwork_e_kernel(
                 in_=w1_scales[:, group, :].rearrange("p (g q t) -> p g t q", t=PACK, q=P),
             )
 
-        def sort_w1(e, g):
-            if g == 0:
-                live["w1"][e] = work.tile([P, H], U32, align_bytes=64, bufs=3, name="w1_sorted")
-            half = slice(g * 512, (g + 1) * 512)
+        def sort_w1(e):
+            live["w1"][e] = work.tile([P, H], U32, align_bytes=64, bufs=3, name="w1_sorted")
             nc.vector.tensor_copy(
-                out=live["w1"][e][:, half].bitcast(I32).rearrange("p (t q) -> p t q", t=PACK),
-                in_=w1_words[:, e, half].bitcast(I32).rearrange("p (q t) -> p t q", t=PACK),
+                out=live["w1"][e][:].bitcast(I32).rearrange("p (g t q) -> p g t q", t=PACK, q=P),
+                in_=w1_words[:, e, :].bitcast(I32).rearrange("p (g q t) -> p g t q", t=PACK, q=P),
             )
 
         def spread(e, k, row):
@@ -152,11 +151,9 @@ def tile_patchwork_e_kernel(
                 stop=True,
             )
 
-        def spread_b2(e):
-            b2_t = psum.tile([P, 2, D], BF16, name="x_t")
-            spread(e, 0, b2_t[:, 0, :])
+        def load_b2(e):
             b2_row = work.tile([P, D], BF16)
-            nc.scalar.copy(out=b2_row[:], in_=b2_t[:, 0, :])
+            nc.sync.dma_start(out=b2_row[:], in_=b2[e].partition_broadcast(P))
             live["b2"][e] = b2_row
 
         def spread_norm(e):
@@ -257,7 +254,7 @@ def tile_patchwork_e_kernel(
                 jobs = [(2 * half + k, slice(0, B), z[:])]
             for t, rows, source in jobs:
                 bias = b1_cols[:, e * H_PASSES + g, t : t + 1]
-                if k == 0 and (n % 4 != 3 or n < 8):
+                if k == 0 and (n < 8 or n % 2 == 0):
                     nc.vector.tensor_scalar(
                         out=r[:, t, rows], in0=source, scalar1=bias, scalar2=0.0, op0=ALU.add, op1=ALU.max
                     )
@@ -402,11 +399,11 @@ def tile_patchwork_e_kernel(
                 if 0 <= n:
                     stage(n, *more)
 
+        load_b2(0)
         turn_b1()
         sort_x(0)
         sort_w1_scales(0)
-        sort_w1(0, 0)
-        sort_w1(0, 1)
+        sort_w1(0)
         sort_x(2)
         for step in range(-2, ITEMS + 13):
             if step >= 0 and step % ROW_TILES == 0:
@@ -416,9 +413,6 @@ def tile_patchwork_e_kernel(
             run(relu, relu_at.get(step, []), 0)
             run(relu, relu_at.get(step, []), 1)
             run(squares, squares_at.get(step, []))
-            for n in add_at.get(step + 1, []):
-                if n % ROW_TILES == 0:
-                    spread_b2(n // ROW_TILES)
             for n in centre_at.get(step, []):
                 if n % ROW_TILES == 0:
                     spread_norm(n // ROW_TILES)
@@ -433,10 +427,10 @@ def tile_patchwork_e_kernel(
             run(quantise_x, turn_at.get(step - 1, []))
             run(scale_plus_beta, scale_at.get(step, []))
             run(centre_times_gamma, centre_at.get(step, []))
-            if step in (0, 1):
-                sort_w1(1, step)
+            if step == 0:
+                sort_w1(1)
             ahead, i = divmod(step + 2, ROW_TILES)
-            if 1 < ahead < NC and i < 2:
-                sort_w1(ahead, i)
+            if 1 < ahead < NC and i == 0:
+                sort_w1(ahead)
             if step == 4:
                 sort_w1_scales(1)

@@ -45,6 +45,7 @@ def tile_patchwork_e_kernel(
         w2_scales = keep.tile([P, NC * H_PASSES // PLANES, D], U8, align_bytes=64)
         b1_rows = keep.tile([P, H // H_PASSES], BF16)
         b1_cols = keep.tile([P, NC * H_PASSES, PACK], F32)
+        b2_rows = keep.tile([P, NC, D], BF16)
         norm_rows = keep.tile([P, 3, D], BF16)
         identity = keep.tile([P, P], F32)
         identity_bf = keep.tile([P, P], BF16)
@@ -152,9 +153,8 @@ def tile_patchwork_e_kernel(
             )
 
         def load_b2(e):
-            b2_row = work.tile([P, D], BF16)
-            nc.sync.dma_start(out=b2_row[:], in_=b2[e].partition_broadcast(P))
-            live["b2"][e] = b2_row
+            nc.sync.dma_start(out=b2_rows[:, e, :], in_=b2[e].partition_broadcast(P))
+            live["b2"][e] = b2_rows[:, e, :]
 
         def spread_norm(e):
             norm = psum.tile([P, 2, D], BF16, bufs=2)
@@ -183,30 +183,38 @@ def tile_patchwork_e_kernel(
             live["x_t"][m] = x_t
 
         def group_x(m):
-            x_grouped = work.tile([P, 2 * P * PACK], BF16, align_bytes=64, bufs=2)
+            half = m % 2
+            if half == 0 or by_halves(m // 2):
+                live["x_grouped"][m] = work.tile([P, 2, 2 * P * PACK], BF16, align_bytes=64, bufs=3, name="x_grouped")
+                live["x_grouped"][m + 1 - half] = live["x_grouped"][m]
+            x_grouped = live["x_grouped"][m]
             nc.scalar.copy(
-                out=x_grouped[:].bitcast(F32).rearrange("q (k b u) -> q k b u", k=2, u=2),
+                out=x_grouped[:, half, :].bitcast(F32).rearrange("q (k b u) -> q k b u", k=2, u=2),
                 in_=live["x_t"][m][:].rearrange("q k u b -> q k b u"),
             )
-            live["x_grouped"][m] = x_grouped
 
         def quantise_x(m):
             e, half = divmod(m, 2)
             if half == 0:
                 live["x_codes"][e] = work.tile([P, B], U32, align_bytes=64, name="x_codes")
                 live["x_scales"][e] = work.tile([P, B], U8, align_bytes=64, name="x_scales")
-            rows = half_rows(half)
+            if by_halves(e):
+                rows, source = half_rows(half), live["x_grouped"][m][:, half, :]
+            elif half == 1:
+                rows, source = slice(0, B), live["x_grouped"][m][:].rearrange("q k n -> q (k n)")
+            else:
+                return
             nc.vector.quantize_mx(
                 out=live["x_codes"][e][:, rows].bitcast(FP8X4),
                 scales=live["x_scales"][e][:, rows],
-                in_=live["x_grouped"][m][:],
+                in_=source,
             )
 
         def half_rows(half):
             return slice(half * 2 * P, (half + 1) * 2 * P)
 
         def by_halves(e):
-            return e < 2 or e == NC - 1
+            return e < 2
 
         def part(n):
             e, i = divmod(n, ROW_TILES)
@@ -305,23 +313,24 @@ def tile_patchwork_e_kernel(
         def add_b2(n):
             e = n // ROW_TILES
             t = work.tile([P, D], F32, bufs=10)
-            t_sum = work.tile([P, 1], F32)
+            if n % 2 == 0:
+                live["t_sum"][n // 2] = work.tile([P, 2], F32, bufs=4, name="t_sum")
             nc.vector.scalar_tensor_tensor(
                 out=t[:],
                 in0=live["y"][n][:],
                 scalar=1.0,
-                in1=live["b2"][e][:],
+                in1=live["b2"][e],
                 op0=ALU.mult,
                 op1=ALU.add,
-                accum_out=t_sum[:],
+                accum_out=live["t_sum"][n // 2][:, n % 2 : n % 2 + 1],
             )
             live["t"][n] = t
-            live["t_sum"][n] = t_sum
 
         def mean(n):
-            neg_mean = work.tile([P, 1], F32, bufs=6)
-            nc.scalar.mul(neg_mean[:], live["t_sum"][n][:], -1.0 / D)
-            live["neg_mean"][n] = neg_mean
+            if n % 2 == 1:
+                neg_mean = work.tile([P, 2], F32, bufs=4)
+                nc.scalar.mul(neg_mean[:], live["t_sum"][n // 2][:], -1.0 / D)
+                live["neg_mean"][n // 2] = neg_mean
 
         def squares(n):
             if n % 2 == 0:
@@ -331,7 +340,7 @@ def tile_patchwork_e_kernel(
                 out=squared[:],
                 in_=live["t"][n][:],
                 func=ACT.Square,
-                bias=live["neg_mean"][n][:],
+                bias=live["neg_mean"][n // 2][:, n % 2 : n % 2 + 1],
                 accum_out=live["sq_sum"][n // 2][:, n % 2 : n % 2 + 1],
             )
 
@@ -349,7 +358,7 @@ def tile_patchwork_e_kernel(
             nc.vector.scalar_tensor_tensor(
                 out=t[:],
                 in0=t[:],
-                scalar=live["neg_mean"][n][:],
+                scalar=live["neg_mean"][n // 2][:, n % 2 : n % 2 + 1],
                 in1=live["norm"][e][:, 0, :],
                 op0=ALU.add,
                 op1=ALU.mult,
@@ -385,9 +394,9 @@ def tile_patchwork_e_kernel(
         second_at = at(7,5)
         add_at = at(7,6)
         mean_at = at(8,7)
-        squares_at = at(8,7)
+        squares_at = at(9,8)
         centre_at = at(9,8)
-        scale_at = at(10,9)
+        scale_at = at(11,10)
 
         turn_at = {-2: [0], -1: [2], 2: [1], 4: [3]}
         for e in range(2, NC):

from contextlib import ExitStack

import concourse.mybir as mybir
from concourse.masks import make_identity

F32 = mybir.dt.float32
BF16 = mybir.dt.bfloat16
I32 = mybir.dt.int32
U32 = mybir.dt.uint32
U8 = mybir.dt.uint8
FP8X4 = mybir.dt.float8_e4m3fn_x4
ALU = mybir.AluOpType
ACT = mybir.ActivationFunctionType

P = 128
PACK = 4
B = 512
NC = 8
APC = 512
H = 1024
D = 512
LN_EPS = 1e-5
ROW_TILES = B // P
H_PASSES = H // (P * PACK)
PLANES = 4
ITEMS = NC * ROW_TILES
FLOPS = 2 * B * NC * (APC * H + H * D)


def tile_patchwork_e_kernel(
    tc, tri, W1_words, W1_scales, b1, W2_words, W2_scales, b2, gamma, beta, out
):
    nc = tc.nc
    with ExitStack() as ctx:
        keep = ctx.enter_context(tc.tile_pool(name="keep", bufs=1))
        work = ctx.enter_context(tc.tile_pool(name="work", bufs=3))
        psum = ctx.enter_context(tc.psum_pool(name="psum", bufs=1))
        ctx.enter_context(tc.manual_schedule())

        tri_sb = keep.tile([P, ROW_TILES, NC * APC], BF16)
        w1_words = keep.tile([P, NC, H], U32, align_bytes=64)
        w2_words = keep.tile([P, NC * H_PASSES, D], U32, align_bytes=64)
        w1_scales = keep.tile([P, NC // PLANES, H], U8, align_bytes=64)
        w1_scales_sorted = keep.tile([P, NC // PLANES, H], U8, align_bytes=64)
        w2_scales = keep.tile([P, NC * H_PASSES // PLANES, D], U8, align_bytes=64)
        b1_rows = keep.tile([P, H // H_PASSES], BF16)
        b1_cols = keep.tile([P, NC * H_PASSES, PACK], F32)
        b2_rows = keep.tile([P, NC, D], BF16)
        norm_rows = keep.tile([P, 3, D], BF16)
        identity = keep.tile([P, P], F32)
        identity_bf = keep.tile([P, P], BF16)
        eps = keep.tile([P, 1], F32)
        table_warm = keep.tile([P, 1], F32)

        nc.vector.memset(b1_rows[:], 0.0)
        nc.vector.memset(eps[:], LN_EPS)
        nc.vector.memset(w1_scales[:].bitcast(I32), 0)
        nc.vector.memset(w2_scales[:].bitcast(I32), 0)
        nc.vector.memset(norm_rows[:].bitcast(I32), 0)
        make_identity(nc, identity[:])
        make_identity(nc, identity_bf[:])
        nc.scalar.activation(out=table_warm[:], in_=eps[:], func=ACT.Abs_reciprocal_sqrt)

        def load_rows(r):
            nc.sync.dma_start(out=tri_sb[:, r, :], in_=tri[r * P : (r + 1) * P, :])

        def load_scales(tile, scales, group):
            for quad in range(4):
                nc.sync.dma_start(
                    out=tile[32 * quad : 32 * quad + 4 * PLANES, group, :].bitcast(I32),
                    in_=scales[PLANES * group : PLANES * (group + 1), 4 * quad : 4 * quad + 4, :].bitcast(I32),
                )

        def load_w1(e):
            nc.sync.dma_start(
                out=w1_words[:, e, :].bitcast(I32),
                in_=W1_words[e].rearrange("p n t -> p (n t)").bitcast(I32),
            )

        def load_w2(e):
            passes = slice(e * H_PASSES, (e + 1) * H_PASSES)
            nc.sync.dma_start(
                out=w2_words[:, passes, :].bitcast(I32),
                in_=W2_words[passes].rearrange("g p n t -> p g (n t)").bitcast(I32),
            )


        nc.sync.dma_start(
            out=b1_rows[: NC * H_PASSES, :], in_=b1.rearrange("e (g c) -> (e g) c", g=H_PASSES)
        )
        load_rows(0)
        load_rows(1)
        load_scales(w1_scales, W1_scales, 0)
        load_w1(0)
        load_w1(1)
        load_rows(2)
        load_rows(3)
        load_scales(w2_scales, W2_scales, 0)
        for k, param in enumerate((b2, gamma, beta)):
            nc.sync.dma_start(out=norm_rows[:NC, k, :], in_=param)
        load_w2(0)
        load_scales(w1_scales, W1_scales, 1)
        for group in range(1, NC * H_PASSES // PLANES):
            load_scales(w2_scales, W2_scales, group)

        def stream_weights(e):
            if e < NC:
                load_w2(e)
                load_b2(e)
            if e + 1 < NC:
                load_w1(e + 1)

        live = {
            name: {}
            for name in (
                "w1", "b2", "norm", "x_sorted", "x_t", "x_grouped", "x_codes", "x_scales", "z", "r", "h_grouped",
                "h_codes", "h_scales", "y", "t", "t_sum", "neg_mean", "sq_sum", "rstd",
            )
        }

        def turn_b1():
            words = b1_rows[:].bitcast(F32)
            b1_t = psum.tile([P, 2, 2, P], F32, name="x_t")
            for u in range(2):
                nc.tensor.transpose(b1_t[:, 0, u, :], words[:, u::2], identity[:])
            nc.vector.tensor_copy(
                out=b1_cols[:].rearrange("q r (u c) -> q r u c", c=2),
                in_=b1_t[:, 0].rearrange("q u r -> q (u r)").bitcast(BF16).rearrange(
                    "q (u r c) -> q r u c", u=2, c=2
                )[:, : NC * H_PASSES],
            )

        def sort_w1_scales(group):
            nc.vector.tensor_copy(
                out=w1_scales_sorted[:, group, :].rearrange("p (g t q) -> p g t q", t=PACK, q=P),
                in_=w1_scales[:, group, :].rearrange("p (g q t) -> p g t q", t=PACK, q=P),
            )

        def sort_w1(e):
            live["w1"][e] = work.tile([P, H], U32, align_bytes=64, bufs=3, name="w1_sorted")
            nc.vector.tensor_copy(
                out=live["w1"][e][:].bitcast(I32).rearrange("p (g t q) -> p g t q", t=PACK, q=P),
                in_=w1_words[:, e, :].bitcast(I32).rearrange("p (g q t) -> p g t q", t=PACK, q=P),
            )

        def spread(e, k, row):
            nc.tensor.matmul(
                row,
                lhsT=identity_bf[:, e : e + 1].to_broadcast([P, P]),
                rhs=norm_rows[:, k, :],
                start=True,
                stop=True,
            )

        def load_b2(e):
            nc.sync.dma_start(out=b2_rows[:, e, :], in_=b2[e].partition_broadcast(P))
            live["b2"][e] = b2_rows[:, e, :]

        def spread_norm(e):
            norm = psum.tile([P, 2, D], BF16, bufs=2)
            for k in range(2):
                spread(e, 1 + k, norm[:, k, :])
            live["norm"][e] = norm

        def sort_x(m):
            e, half = divmod(m, 2)
            x_sorted = work.tile([P, 2, APC], BF16)
            for k in range(2):
                view = x_sorted[:, k, :].rearrange("b (u q c) -> b u q c", u=2, c=2)
                source = tri_sb[:, 2 * half + k, :].rearrange("b (q u c e) -> b e u q c", u=2, c=2, e=NC)[:, e]
                if m == 0 and k == 1:
                    nc.vector.tensor_copy(out=view, in_=source)
                else:
                    nc.gpsimd.tensor_scalar(out=view, in0=source, scalar1=1.0, scalar2=0.0, op0=ALU.mult, op1=ALU.add)
            live["x_sorted"][m] = x_sorted

        def transpose_x(m):
            x_t = psum.tile([P, 2, 2, P], F32)
            for k in range(2):
                words = live["x_sorted"][m][:, k, :].bitcast(F32)
                for u in range(2):
                    nc.tensor.transpose(x_t[:, k, u, :], words[:, u * P : (u + 1) * P], identity[:])
            live["x_t"][m] = x_t

        def group_x(m):
            half = m % 2
            if half == 0 or by_halves(m // 2):
                live["x_grouped"][m] = work.tile([P, 2, 2 * P * PACK], BF16, align_bytes=64, bufs=3, name="x_grouped")
                live["x_grouped"][m + 1 - half] = live["x_grouped"][m]
            x_grouped = live["x_grouped"][m]
            nc.scalar.copy(
                out=x_grouped[:, half, :].bitcast(F32).rearrange("q (k b u) -> q k b u", k=2, u=2),
                in_=live["x_t"][m][:].rearrange("q k u b -> q k b u"),
            )

        def quantise_x(m):
            e, half = divmod(m, 2)
            if half == 0:
                live["x_codes"][e] = work.tile([P, B], U32, align_bytes=64, name="x_codes")
                live["x_scales"][e] = work.tile([P, B], U8, align_bytes=64, name="x_scales")
            if by_halves(e):
                rows, source = half_rows(half), live["x_grouped"][m][:, half, :]
            elif half == 1:
                rows, source = slice(0, B), live["x_grouped"][m][:].rearrange("q k n -> q (k n)")
            else:
                return
            nc.vector.quantize_mx(
                out=live["x_codes"][e][:, rows].bitcast(FP8X4),
                scales=live["x_scales"][e][:, rows],
                in_=source,
            )

        def half_rows(half):
            return slice(half * 2 * P, (half + 1) * 2 * P)

        def by_halves(e):
            return e < 2

        def part(n):
            e, i = divmod(n, ROW_TILES)
            major, minor = divmod(i, 2)
            return (minor, major) if by_halves(e) else (major, minor)

        def mx(e, j, rows, z):
            group, plane = divmod(e, PLANES)
            cols = slice(j * P, (j + 1) * P)
            nc.tensor.matmul_mx(
                out=z,
                lhsT=live["w1"][e][:, cols].bitcast(FP8X4),
                lhsT_scale=w1_scales_sorted[4 * plane : P, group, cols],
                rhs=live["x_codes"][e][:, rows].bitcast(FP8X4),
                rhs_scale=live["x_scales"][e][:, rows],
                start=True,
                stop=True,
            )

        def first_matmul(n):
            e = n // ROW_TILES
            g, half = part(n)
            banks = []
            for k in range(2):
                z = psum.tile([P, B], F32, bufs=3)
                if by_halves(e):
                    for c in range(2):
                        mx(e, PACK * g + 2 * k + c, half_rows(half), z[:, half_rows(c)])
                else:
                    mx(e, PACK * g + 2 * half + k, slice(0, B), z[:])
                banks.append(z)
            live["z"][n] = banks

        def relu(n, k):
            e = n // ROW_TILES
            g, half = part(n)
            key = (e, g, half) if by_halves(e) else (e, g)
            if key not in live["r"]:
                live["r"][key] = work.tile([P, PACK, B], F32, name="r")
            r = live["r"][key]
            z = live["z"][n][k]
            if by_halves(e):
                jobs = [(2 * k + c, half_rows(half), z[:, half_rows(c)]) for c in range(2)]
            else:
                jobs = [(2 * half + k, slice(0, B), z[:])]
            for t, rows, source in jobs:
                bias = b1_cols[:, e * H_PASSES + g, t : t + 1]
                if k == 0 and (n < 8 or n % 2 == 0):
                    nc.vector.tensor_scalar(
                        out=r[:, t, rows], in0=source, scalar1=bias, scalar2=0.0, op0=ALU.add, op1=ALU.max
                    )
                else:
                    nc.scalar.activation(out=r[:, t, rows], in_=source, func=ACT.Relu, bias=bias)

        def square(n):
            e = n // ROW_TILES
            g, half = part(n)
            key = (e, g, half) if by_halves(e) else (e, g)
            h_grouped = work.tile([P, 2 * P, PACK], BF16, align_bytes=64)
            r = live["r"][key]
            source = r[:, :, half_rows(half)].rearrange("q t (c i) -> q c t i", i=4)
            target = h_grouped[:].rearrange("q (c i) t -> q c t i", i=4)
            nc.scalar.activation(out=target, in_=source, func=ACT.Square)
            live["h_grouped"][n] = h_grouped

        def quantise_h(n):
            e, i = divmod(n, ROW_TILES)
            g, half = part(n)
            if i == 0:
                live["h_codes"][e] = work.tile([P, H_PASSES, B], U32, align_bytes=64, name="h_codes")
                live["h_scales"][e] = work.tile([P, H_PASSES, B], U8, align_bytes=64, name="h_scales")
            rows = half_rows(half)
            nc.vector.quantize_mx(
                out=live["h_codes"][e][:, g, rows].bitcast(FP8X4),
                scales=live["h_scales"][e][:, g, rows],
                in_=live["h_grouped"][n][:].rearrange("q b t -> q (b t)"),
            )

        def second_matmul(n):
            e, r = divmod(n, ROW_TILES)
            rows = slice(r * P, (r + 1) * P)
            y = psum.tile([P, D], F32, bufs=2)
            for g in range(H_PASSES):
                group, plane = divmod(e * H_PASSES + g, PLANES)
                nc.tensor.matmul_mx(
                    out=y[:],
                    lhsT=live["h_codes"][e][:, g, rows].bitcast(FP8X4),
                    lhsT_scale=live["h_scales"][e][:, g, rows],
                    rhs=w2_words[:, e * H_PASSES + g, :].bitcast(FP8X4),
                    rhs_scale=w2_scales[4 * plane : P, group, :],
                    start=(g == 0),
                    stop=(g == H_PASSES - 1),
                )
            live["y"][n] = y

        def add_b2(n):
            e = n // ROW_TILES
            t = work.tile([P, D], F32, bufs=10)
            if n % 2 == 0:
                live["t_sum"][n // 2] = work.tile([P, 2], F32, bufs=4, name="t_sum")
            nc.vector.scalar_tensor_tensor(
                out=t[:],
                in0=live["y"][n][:],
                scalar=1.0,
                in1=live["b2"][e],
                op0=ALU.mult,
                op1=ALU.add,
                accum_out=live["t_sum"][n // 2][:, n % 2 : n % 2 + 1],
            )
            live["t"][n] = t

        def mean(n):
            if n % 2 == 1:
                neg_mean = work.tile([P, 2], F32, bufs=4)
                nc.scalar.mul(neg_mean[:], live["t_sum"][n // 2][:], -1.0 / D)
                live["neg_mean"][n // 2] = neg_mean

        def squares(n):
            if n % 2 == 0:
                live["sq_sum"][n // 2] = work.tile([P, 2], F32, name="sq_sum")
            squared = work.tile([P, D], BF16)
            nc.scalar.activation(
                out=squared[:],
                in_=live["t"][n][:],
                func=ACT.Square,
                bias=live["neg_mean"][n // 2][:, n % 2 : n % 2 + 1],
                accum_out=live["sq_sum"][n // 2][:, n % 2 : n % 2 + 1],
            )

        def inverse_deviation(n):
            if n % 2 == 1:
                rstd = work.tile([P, 2], F32)
                nc.scalar.activation(
                    out=rstd[:], in_=live["sq_sum"][n // 2][:], func=ACT.Abs_reciprocal_sqrt, scale=1.0 / D, bias=eps[:]
                )
                live["rstd"][n // 2] = rstd

        def centre_times_gamma(n):
            e = n // ROW_TILES
            t = live["t"][n]
            nc.vector.scalar_tensor_tensor(
                out=t[:],
                in0=t[:],
                scalar=live["neg_mean"][n // 2][:, n % 2 : n % 2 + 1],
                in1=live["norm"][e][:, 0, :],
                op0=ALU.add,
                op1=ALU.mult,
            )

        def scale_plus_beta(n):
            e, r = divmod(n, ROW_TILES)
            t = live["t"][n]
            nc.vector.scalar_tensor_tensor(
                out=t[:],
                in0=t[:],
                scalar=live["rstd"][n // 2][:, n % 2 : n % 2 + 1],
                in1=live["norm"][e][:, 1, :],
                op0=ALU.mult,
                op1=ALU.add,
            )
            nc.sync.dma_start(out=out[r * P : (r + 1) * P, e * D : (e + 1) * D], in_=t[:])

        order = [0, 1, 4, 5, 2, 3, 6, 7] + list(range(2 * ROW_TILES, ITEMS))

        def at(lag_normal, lag_halves):
            steps = {}
            for place, n in enumerate(order):
                lag = lag_halves if by_halves(n // ROW_TILES) else lag_normal
                steps.setdefault(place + lag, []).append(n)
            return steps

        multiply_at = at(0, 0)

        relu_at = at(1, 1)
        square_at = at(3,2)
        quantise_h_at = at(4,3)
        second_at = at(7,5)
        add_at = at(7,6)
        mean_at = at(8,7)
        squares_at = at(9,8)
        centre_at = at(9,8)
        scale_at = at(11,10)

        turn_at = {-2: [0], -1: [2], 2: [1], 4: [3]}
        for e in range(2, NC):
            turn_at[ROW_TILES * e - 3] = [2 * e]
            turn_at[ROW_TILES * e - 2] = [2 * e + 1]

        def run(stage, items, *more):
            for n in items:
                if 0 <= n:
                    stage(n, *more)

        load_b2(0)
        turn_b1()
        sort_x(0)
        sort_w1_scales(0)
        sort_w1(0)
        sort_x(2)
        for step in range(-2, ITEMS + 13):
            if step >= 0 and step % ROW_TILES == 0:
                stream_weights(step // ROW_TILES + 1)
            run(mean, mean_at.get(step, []))
            run(sort_x, turn_at.get(step + 2, []) if step >= 0 else [])
            run(relu, relu_at.get(step, []), 0)
            run(relu, relu_at.get(step, []), 1)
            run(squares, squares_at.get(step, []))
            for n in centre_at.get(step, []):
                if n % ROW_TILES == 0:
                    spread_norm(n // ROW_TILES)
            run(second_matmul, second_at.get(step, []))
            run(first_matmul, multiply_at.get(step, []))
            run(transpose_x, turn_at.get(step, []))
            run(square, square_at.get(step, []))
            run(inverse_deviation, squares_at.get(step, []))
            run(group_x, turn_at.get(step, []))
            run(add_b2, add_at.get(step, []))
            run(quantise_h, quantise_h_at.get(step, []))
            run(quantise_x, turn_at.get(step - 1, []))
            run(scale_plus_beta, scale_at.get(step, []))
            run(centre_times_gamma, centre_at.get(step, []))
            if step == 0:
                sort_w1(1)
            ahead, i = divmod(step + 2, ROW_TILES)
            if 1 < ahead < NC and i == 0:
                sort_w1(ahead)
            if step == 4:
                sort_w1_scales(1)
